import numpy as np
import ml_dtypes


def mxq(x, axis, fmt="e4m3"):
    dtype, down = {"e4m3": (ml_dtypes.float8_e4m3fn, 7), "e5m2": (ml_dtypes.float8_e5m2, 14)}[fmt]
    v = np.moveaxis(np.asarray(x, np.float32).astype(ml_dtypes.bfloat16).astype(np.float64), axis, -1)
    blocks = v.reshape(v.shape[:-1] + (-1, 32))
    amax = np.abs(blocks).max(-1, keepdims=True)
    byte = np.maximum(np.where(amax > 0, np.frexp(amax)[1] - 1 + 127, 0) - down, 1)
    scale = np.exp2(byte - 127.0)
    codes = (blocks / scale).astype(np.float32).astype(dtype).astype(np.float64)
    return np.moveaxis((codes * scale).reshape(v.shape), -1, axis)


WIDE = False


def mx_kscale(k):
    if not WIDE:
        return np.ones(k)
    levels = np.array([10, -10, 5, -5, 0])
    a = np.random.permutation(np.resize(levels, k // 512 * 4)).reshape(k // 512, 4)
    idx = np.arange(k)
    return np.exp2(a[idx // 512, idx % 128 // 32])


BF16 = ml_dtypes.bfloat16


def bf(x):
    return np.asarray(x, np.float32).astype(BF16)


def f64(x):
    return np.asarray(x).astype(np.float64)


E2M1 = np.array([0.0, 0.5, 1.0, 1.5, 2.0, 3.0, 4.0, 6.0, -0.0, -0.5, -1.0, -1.5, -2.0, -3.0, -4.0, -6.0])


def pack_weight(w, fmt):
    k, n = w.shape
    w = f64(bf(w)).reshape(k // 32, 32, n)
    amax = np.abs(w).max(1)
    if fmt == "e4m3":
        byte = np.frexp(amax)[1] - 1 + 127 - 7
    else:
        mant, ex = np.frexp(amax / 6.0)
        byte = np.where(mant > 0.5, ex, ex - 1) + 127
    byte = np.clip(np.where(amax > 0, byte, 1), 1, 254)
    scaled = (w * np.exp2(127.0 - byte)[:, None, :]).reshape(k, n).astype(np.float32)
    by_word = np.ascontiguousarray(scaled.reshape(k // 512, 128, 4, n).transpose(0, 1, 3, 2))
    if fmt == "e4m3":
        words = by_word.astype(ml_dtypes.float8_e4m3fn).view(np.uint8)
    else:
        c = by_word.astype(ml_dtypes.float4_e2m1fn).view(np.uint8) & 0xF
        words = c[..., 0::2] | (c[..., 1::2] << 4)
    return np.ascontiguousarray(words), np.ascontiguousarray(byte.astype(np.uint8).reshape(k // 512, 16, n))


def unpack_weight(words, scales, fmt):
    g, p, n, _ = words.shape
    if fmt == "e4m3":
        vals = np.ascontiguousarray(words).view(ml_dtypes.float8_e4m3fn).astype(np.float64)
    else:
        nib = np.empty((g, p, n, 4), np.uint8)
        nib[..., 0::2] = words & 0xF
        nib[..., 1::2] = words >> 4
        vals = E2M1[nib]
    vals = vals * np.repeat(np.exp2(scales.astype(np.float64) - 127.0), 8, axis=1)[..., None]
    return vals.transpose(0, 1, 3, 2).reshape(g * 512, n)


B, SIDE, HE, Z, HD, XO = 4096, 32, 1024, 512, 1024, 512
FMT = "e4m3"


def setup_inputs():
    n = np.random.standard_normal
    s = mx_kscale(HD)
    hd = bf(np.tanh(n((B, HD))) * s)
    w_mu = n((XO, HD)) * 1.5 / np.sqrt(HD) / s[None, :]
    mu_words, mu_scales = pack_weight(np.ascontiguousarray(w_mu.T), FMT)
    b_mu_d = bf(n(XO) * 0.3)
    w_ls = n((XO, HD)) * 1.5 / np.sqrt(HD) / s[None, :]
    ls_words, ls_scales = pack_weight(np.ascontiguousarray(w_ls.T), FMT)
    b_ls_d = bf(n(XO) * 0.3)
    eps_x = bf(n((B, XO)))
    return {"hd": hd,
            "W_mu_d_words": mu_words,
            "W_mu_d_scales": mu_scales,
            "b_mu_d": b_mu_d,
            "W_ls_d_words": ls_words,
            "W_ls_d_scales": ls_scales,
            "b_ls_d": b_ls_d,
            "eps_x": eps_x}


def reference(hd, W_mu_d_words, W_mu_d_scales, b_mu_d, W_ls_d_words, W_ls_d_scales, b_ls_d, eps_x):
    hq = mxq(f64(hd), 1, "e4m3")
    mu_d = (hq @ unpack_weight(W_mu_d_words, W_mu_d_scales, FMT)) + f64(b_mu_d)
    ls_d = (hq @ unpack_weight(W_ls_d_words, W_ls_d_scales, FMT)) + f64(b_ls_d)
    return mu_d + np.exp(0.5 * ls_d) * f64(eps_x)

@@ -1,0 +1,154 @@
+from contextlib import ExitStack
+
+import concourse.mybir as mybir
+from concourse.masks import make_identity
+
+F32 = mybir.dt.float32
+BF16 = mybir.dt.bfloat16
+I32 = mybir.dt.int32
+U32 = mybir.dt.uint32
+U8 = mybir.dt.uint8
+FP8X4 = mybir.dt.float8_e4m3fn_x4
+ADD = mybir.AluOpType.add
+MULT = mybir.AluOpType.mult
+EXP = mybir.ActivationFunctionType.Exp
+
+P = 128
+ROWS, K, N = 4096, 1024, 512
+PACK = 4
+PASSES = K // (P * PACK)
+PAIRS = 2
+ROW_TILES = 4
+BLOCK = P * ROW_TILES
+BLOCKS = ROWS // BLOCK
+MU, LS = 0, 1
+QUADRANTS = 4
+
+FLOPS = 2 * ROWS * K * (2 * N)
+
+
+def tile_vae_pb_t_kernel(
+    tc, hd, W_mu_d_words, W_mu_d_scales, b_mu_d, W_ls_d_words, W_ls_d_scales, b_ls_d, eps_x, out
+):
+    nc = tc.nc
+    hd_blocks = hd.rearrange("(b p t) k -> b p t k", p=P, t=ROW_TILES)
+    eps_blocks = eps_x.rearrange("(b p t) n -> b p t n", p=P, t=ROW_TILES)
+    out_blocks = out.rearrange("(b p t) n -> b p t n", p=P, t=ROW_TILES)
+
+    with ExitStack() as ctx:
+        consts = ctx.enter_context(tc.tile_pool(name="consts", bufs=1))
+        resident = ctx.enter_context(tc.tile_pool(name="resident", bufs=1))
+        stage = ctx.enter_context(tc.tile_pool(name="stage", bufs=2))
+        work = ctx.enter_context(tc.tile_pool(name="work", bufs=3))
+        psum_turn = ctx.enter_context(tc.psum_pool(name="psum_turn", bufs=2))
+        psum_acc = ctx.enter_context(tc.psum_pool(name="psum_acc", bufs=3))
+
+        ident = consts.tile([P, P], F32, name="ident")
+        make_identity(nc, ident[:])
+
+        w_planes = consts.tile([P, 2, PASSES, N], U8, name="w_planes", align_bytes=64)
+        nc.vector.memset(w_planes[:].bitcast(I32), 0)
+        w_words = consts.tile([P, 2, PASSES, N], U32, name="w_words", align_bytes=64)
+        bias = consts.tile([P, 2, N], BF16, name="bias")
+
+        hd_sb = [resident.tile([P, ROW_TILES, K], BF16, name="hd%d" % b) for b in range(BLOCKS)]
+        eps_sb = [resident.tile([P, ROW_TILES, N], BF16, name="eps%d" % b) for b in range(BLOCKS)]
+
+        nc.sync.dma_start(out=hd_sb[0][:], in_=hd_blocks[0])
+        for w, scales in ((MU, W_mu_d_scales), (LS, W_ls_d_scales)):
+            for q in range(QUADRANTS):
+                nc.sync.dma_start(
+                    out=w_planes[32 * q : 32 * q + 4, w, :, :].bitcast(I32),
+                    in_=scales[:, 4 * q : 4 * q + 4, :].rearrange("g r n -> r g n").bitcast(I32),
+                )
+        for w, words in ((MU, W_mu_d_words), (LS, W_ls_d_words)):
+            nc.sync.dma_start(
+                out=w_words[:, w, :, :].bitcast(I32),
+                in_=words.rearrange("g p n t -> p g (n t)").bitcast(I32),
+            )
+        nc.sync.dma_start(out=bias[:, MU, :], in_=b_mu_d.partition_broadcast(P))
+        nc.sync.dma_start(out=bias[:, LS, :], in_=b_ls_d.partition_broadcast(P))
+        nc.sync.dma_start(out=eps_sb[0][:], in_=eps_blocks[0])
+        for b in range(1, BLOCKS):
+            nc.sync.dma_start(out=hd_sb[b][:], in_=hd_blocks[b])
+            nc.sync.dma_start(out=eps_sb[b][:], in_=eps_blocks[b])
+
+        def turn_block(b):
+            grouped = stage.tile([P, PASSES * BLOCK * PACK], BF16, name="grouped", align_bytes=64)
+            grouped_words = grouped[:].bitcast(F32).rearrange(
+                "p (g c u) -> p g c u", g=PASSES, c=BLOCK, u=PAIRS
+            )
+            for t in range(ROW_TILES):
+                hd_words = hd_sb[b][:, t, :].bitcast(F32)
+                turned = psum_turn.tile([P, PASSES * PAIRS, P], F32, name="turned")
+                for g in range(PASSES):
+                    for u in range(PAIRS):
+                        words_of_pass = slice(g * P * PAIRS + u, (g + 1) * P * PAIRS, PAIRS)
+                        nc.tensor.transpose(
+                            turned[:, g * PAIRS + u, :],
+                            hd_words[:, words_of_pass],
+                            ident[:],
+                        )
+                nc.scalar.copy(
+                    out=grouped_words[:, :, t * P : (t + 1) * P, :],
+                    in_=turned[:].rearrange("p (g u) c -> p g c u", u=PAIRS),
+                )
+            return grouped
+
+        def quantise_block(grouped):
+            codes = stage.tile([P, PASSES, BLOCK], U32, name="codes", align_bytes=64)
+            hd_planes = stage.tile([P, PASSES, BLOCK], U8, name="hd_planes", align_bytes=64)
+            nc.vector.quantize_mx(
+                out=codes[:].rearrange("p g c -> p (g c)").bitcast(FP8X4),
+                scales=hd_planes[:].rearrange("p g c -> p (g c)"),
+                in_=grouped[:],
+            )
+            return codes, hd_planes
+
+        def product(w, codes, hd_planes, t, acc):
+            cols = slice(t * P, (t + 1) * P)
+            for g in range(PASSES):
+                nc.tensor.matmul_mx(
+                    out=acc[:],
+                    lhsT=codes[:, g, cols].bitcast(FP8X4),
+                    lhsT_scale=hd_planes[:, g, cols],
+                    rhs=w_words[:, w, g, :].bitcast(FP8X4),
+                    rhs_scale=w_planes[:, w, g, :],
+                    start=(g == 0),
+                    stop=(g == PASSES - 1),
+                )
+
+        def front(codes, hd_planes, t):
+            ls_acc = psum_acc.tile([P, N], F32, name="ls_acc")
+            product(LS, codes, hd_planes, t, ls_acc)
+            mu_acc = psum_acc.tile([P, N], F32, name="mu_acc")
+            product(MU, codes, hd_planes, t, mu_acc)
+            log_var = work.tile([P, N], F32, name="log_var")
+            nc.vector.tensor_tensor(out=log_var[:], in0=ls_acc[:], in1=bias[:, LS, :], op=ADD)
+            std = work.tile([P, N], F32, name="std")
+            nc.scalar.activation(out=std[:], in_=log_var[:], func=EXP, scale=0.5)
+            return mu_acc, std
+
+        def back(b, t, mu_acc, std):
+            noise = work.tile([P, N], F32, name="noise")
+            nc.vector.tensor_tensor(out=noise[:], in0=std[:], in1=eps_sb[b][:, t, :], op=MULT)
+            summed = work.tile([P, N], F32, name="summed")
+            nc.vector.tensor_tensor(out=summed[:], in0=mu_acc[:], in1=noise[:], op=ADD)
+            result = work.tile([P, N], F32, name="result")
+            nc.vector.tensor_tensor(out=result[:], in0=summed[:], in1=bias[:, MU, :], op=ADD)
+            nc.sync.dma_start(out=out_blocks[b][:, t, :], in_=result[:])
+
+        with tc.manual_schedule():
+            operands = quantise_block(turn_block(0))
+            waiting = None
+            for b in range(BLOCKS):
+                grouped = turn_block(b + 1) if b + 1 < BLOCKS else None
+                codes, hd_planes = operands
+                for t in range(ROW_TILES):
+                    mu_acc, std = front(codes, hd_planes, t)
+                    if waiting is not None:
+                        back(*waiting)
+                    waiting = (b, t, mu_acc, std)
+                if grouped is not None:
+                    operands = quantise_block(grouped)
+            back(*waiting)

@@ -21,6 +21,7 @@ PAIRS = 2
 ROW_TILES = 4
 BLOCK = P * ROW_TILES
 BLOCKS = ROWS // BLOCK
+N_TILES = N // P
 MU, LS = 0, 1
 QUADRANTS = 4
 
@@ -39,9 +40,9 @@ def tile_vae_pb_t_kernel(
         consts = ctx.enter_context(tc.tile_pool(name="consts", bufs=1))
         resident = ctx.enter_context(tc.tile_pool(name="resident", bufs=1))
         stage = ctx.enter_context(tc.tile_pool(name="stage", bufs=2))
-        work = ctx.enter_context(tc.tile_pool(name="work", bufs=3))
-        psum_turn = ctx.enter_context(tc.psum_pool(name="psum_turn", bufs=2))
-        psum_acc = ctx.enter_context(tc.psum_pool(name="psum_acc", bufs=3))
+        work = ctx.enter_context(tc.tile_pool(name="work", bufs=4))
+        psum_turn = ctx.enter_context(tc.psum_pool(name="psum_turn", bufs=4))
+        psum_rows = ctx.enter_context(tc.psum_pool(name="psum_rows", bufs=2))
 
         ident = consts.tile([P, P], F32, name="ident")
         make_identity(nc, ident[:])
@@ -49,29 +50,37 @@ def tile_vae_pb_t_kernel(
         w_planes = consts.tile([P, 2, PASSES, N], U8, name="w_planes", align_bytes=64)
         nc.vector.memset(w_planes[:].bitcast(I32), 0)
         w_words = consts.tile([P, 2, PASSES, N], U32, name="w_words", align_bytes=64)
-        bias = consts.tile([P, 2, N], BF16, name="bias")
+        b_mu_rows = consts.tile([P, N], BF16, name="b_mu_rows")
+        b_ls_tiles = consts.tile([P, P], BF16, name="b_ls_tiles")
+        nc.vector.memset(b_ls_tiles[:], 0.0)
+
+        warm = consts.tile([P, 1], F32, name="warm")
+        nc.vector.memset(warm[:], 0.0)
+        nc.scalar.activation(out=warm[:], in_=warm[:], func=EXP)
 
         hd_sb = [resident.tile([P, ROW_TILES, K], BF16, name="hd%d" % b) for b in range(BLOCKS)]
         eps_sb = [resident.tile([P, ROW_TILES, N], BF16, name="eps%d" % b) for b in range(BLOCKS)]
 
         nc.sync.dma_start(out=hd_sb[0][:], in_=hd_blocks[0])
-        for w, scales in ((MU, W_mu_d_scales), (LS, W_ls_d_scales)):
+        nc.sync.dma_start(out=b_ls_tiles[0:N_TILES, :], in_=b_ls_d.rearrange("(j c) -> j c", c=P))
+        for w, scales in ((LS, W_ls_d_scales), (MU, W_mu_d_scales)):
             for q in range(QUADRANTS):
                 nc.sync.dma_start(
                     out=w_planes[32 * q : 32 * q + 4, w, :, :].bitcast(I32),
                     in_=scales[:, 4 * q : 4 * q + 4, :].rearrange("g r n -> r g n").bitcast(I32),
                 )
-        for w, words in ((MU, W_mu_d_words), (LS, W_ls_d_words)):
+        for w, words in ((LS, W_ls_d_words), (MU, W_mu_d_words)):
             nc.sync.dma_start(
                 out=w_words[:, w, :, :].bitcast(I32),
                 in_=words.rearrange("g p n t -> p g (n t)").bitcast(I32),
             )
-        nc.sync.dma_start(out=bias[:, MU, :], in_=b_mu_d.partition_broadcast(P))
-        nc.sync.dma_start(out=bias[:, LS, :], in_=b_ls_d.partition_broadcast(P))
+        nc.sync.dma_start(out=hd_sb[1][:], in_=hd_blocks[1])
         nc.sync.dma_start(out=eps_sb[0][:], in_=eps_blocks[0])
-        for b in range(1, BLOCKS):
+        nc.sync.dma_start(out=b_mu_rows[:], in_=b_mu_d.partition_broadcast(P))
+        for b in range(2, BLOCKS):
             nc.sync.dma_start(out=hd_sb[b][:], in_=hd_blocks[b])
-            nc.sync.dma_start(out=eps_sb[b][:], in_=eps_blocks[b])
+            nc.sync.dma_start(out=eps_sb[b - 1][:], in_=eps_blocks[b - 1])
+        nc.sync.dma_start(out=eps_sb[BLOCKS - 1][:], in_=eps_blocks[BLOCKS - 1])
 
         def turn_block(b):
             grouped = stage.tile([P, PASSES * BLOCK * PACK], BF16, name="grouped", align_bytes=64)
@@ -80,7 +89,7 @@ def tile_vae_pb_t_kernel(
             )
             for t in range(ROW_TILES):
                 hd_words = hd_sb[b][:, t, :].bitcast(F32)
-                turned = psum_turn.tile([P, PASSES * PAIRS, P], F32, name="turned")
+                turned = psum_turn.tile([P, PASSES * PAIRS, P], F32, name="turned", tag="turn")
                 for g in range(PASSES):
                     for u in range(PAIRS):
                         words_of_pass = slice(g * P * PAIRS + u, (g + 1) * P * PAIRS, PAIRS)
@@ -105,50 +114,89 @@ def tile_vae_pb_t_kernel(
             )
             return codes, hd_planes
 
-        def product(w, codes, hd_planes, t, acc):
-            cols = slice(t * P, (t + 1) * P)
-            for g in range(PASSES):
-                nc.tensor.matmul_mx(
-                    out=acc[:],
-                    lhsT=codes[:, g, cols].bitcast(FP8X4),
-                    lhsT_scale=hd_planes[:, g, cols],
-                    rhs=w_words[:, w, g, :].bitcast(FP8X4),
-                    rhs_scale=w_planes[:, w, g, :],
-                    start=(g == 0),
-                    stop=(g == PASSES - 1),
+        def half_bias_per_partition():
+            halved = consts.tile([P, P], F32, name="halved")
+            nc.vector.tensor_scalar(
+                out=halved[:], in0=b_ls_tiles[:], scalar1=0.5, scalar2=None, op0=MULT
+            )
+            turned = psum_turn.tile([P, P], F32, name="bias_turned", tag="turn")
+            nc.tensor.transpose(turned[:], halved[:], ident[:])
+            half_b_ls = consts.tile([P, N_TILES], F32, name="half_b_ls")
+            nc.vector.tensor_copy(out=half_b_ls[:], in_=turned[:, 0:N_TILES])
+            return half_b_ls
+
+        def std_of_block(codes, hd_planes, half_b_ls):
+            std_turned = stage.tile([P, N_TILES, BLOCK], F32, name="std_turned")
+            for j in range(N_TILES):
+                cols = slice(j * P, (j + 1) * P)
+                ls_turned = psum_turn.tile([P, BLOCK], F32, name="ls_turned", tag="turn")
+                for g in range(PASSES):
+                    nc.tensor.matmul_mx(
+                        out=ls_turned[:],
+                        lhsT=w_words[:, LS, g, cols].bitcast(FP8X4),
+                        lhsT_scale=w_planes[:, LS, g, cols],
+                        rhs=codes[:, g, :].bitcast(FP8X4),
+                        rhs_scale=hd_planes[:, g, :],
+                        start=(g == 0),
+                        stop=(g == PASSES - 1),
+                    )
+                nc.scalar.activation(
+                    out=std_turned[:, j, :],
+                    in_=ls_turned[:],
+                    func=EXP,
+                    bias=half_b_ls[:, j : j + 1],
+                    scale=0.5,
                 )
+            return std_turned
 
-        def front(codes, hd_planes, t):
-            ls_acc = psum_acc.tile([P, N], F32, name="ls_acc")
-            product(LS, codes, hd_planes, t, ls_acc)
-            mu_acc = psum_acc.tile([P, N], F32, name="mu_acc")
-            product(MU, codes, hd_planes, t, mu_acc)
-            log_var = work.tile([P, N], F32, name="log_var")
-            nc.vector.tensor_tensor(out=log_var[:], in0=ls_acc[:], in1=bias[:, LS, :], op=ADD)
-            std = work.tile([P, N], F32, name="std")
-            nc.scalar.activation(out=std[:], in_=log_var[:], func=EXP, scale=0.5)
-            return mu_acc, std
-
-        def back(b, t, mu_acc, std):
-            noise = work.tile([P, N], F32, name="noise")
-            nc.vector.tensor_tensor(out=noise[:], in0=std[:], in1=eps_sb[b][:, t, :], op=MULT)
-            summed = work.tile([P, N], F32, name="summed")
-            nc.vector.tensor_tensor(out=summed[:], in0=mu_acc[:], in1=noise[:], op=ADD)
-            result = work.tile([P, N], F32, name="result")
-            nc.vector.tensor_tensor(out=result[:], in0=summed[:], in1=bias[:, MU, :], op=ADD)
-            nc.sync.dma_start(out=out_blocks[b][:, t, :], in_=result[:])
+        def finish_row_tiles(b, tiles, codes, hd_planes, std_turned):
+            std_acc = {}
+            mu_acc = {}
+            noise = {}
+            for t in tiles:
+                std_acc[t] = psum_rows.tile([P, N], F32, name="std_acc")
+                for j in range(N_TILES):
+                    nc.tensor.transpose(
+                        std_acc[t][:, j * P : (j + 1) * P],
+                        std_turned[:, j, t * P : (t + 1) * P],
+                        ident[:],
+                    )
+            for t in tiles:
+                cols = slice(t * P, (t + 1) * P)
+                mu_acc[t] = psum_rows.tile([P, N], F32, name="mu_acc")
+                for g in range(PASSES):
+                    nc.tensor.matmul_mx(
+                        out=mu_acc[t][:],
+                        lhsT=codes[:, g, cols].bitcast(FP8X4),
+                        lhsT_scale=hd_planes[:, g, cols],
+                        rhs=w_words[:, MU, g, :].bitcast(FP8X4),
+                        rhs_scale=w_planes[:, MU, g, :],
+                        start=(g == 0),
+                        stop=(g == PASSES - 1),
+                    )
+            for t in tiles:
+                noise[t] = work.tile([P, N], F32, name="noise")
+                nc.vector.tensor_tensor(
+                    out=noise[t][:], in0=std_acc[t][:], in1=eps_sb[b][:, t, :], op=MULT
+                )
+            for t in tiles:
+                summed = work.tile([P, N], F32, name="summed")
+                nc.vector.tensor_tensor(out=summed[:], in0=mu_acc[t][:], in1=noise[t][:], op=ADD)
+                result = work.tile([P, N], F32, name="result")
+                nc.gpsimd.tensor_tensor(out=result[:], in0=summed[:], in1=b_mu_rows[:], op=ADD)
+                nc.sync.dma_start(out=out_blocks[b][:, t, :], in_=result[:])
 
         with tc.manual_schedule():
-            operands = quantise_block(turn_block(0))
-            waiting = None
+            grouped = {0: turn_block(0)}
+            operands = {0: quantise_block(grouped[0])}
+            half_b_ls = half_bias_per_partition()
+            grouped[1] = turn_block(1)
             for b in range(BLOCKS):
-                grouped = turn_block(b + 1) if b + 1 < BLOCKS else None
-                codes, hd_planes = operands
-                for t in range(ROW_TILES):
-                    mu_acc, std = front(codes, hd_planes, t)
-                    if waiting is not None:
-                        back(*waiting)
-                    waiting = (b, t, mu_acc, std)
-                if grouped is not None:
-                    operands = quantise_block(grouped)
-            back(*waiting)
+                codes, hd_planes = operands[b]
+                std_turned = std_of_block(codes, hd_planes, half_b_ls)
+                if b + 2 < BLOCKS:
+                    grouped[b + 2] = turn_block(b + 2)
+                finish_row_tiles(b, (0, 1), codes, hd_planes, std_turned)
+                if b + 1 < BLOCKS:
+                    operands[b + 1] = quantise_block(grouped[b + 1])
+                finish_row_tiles(b, (2, 3), codes, hd_planes, std_turned)

@@ -40,6 +40,7 @@ def tile_vae_pb_t_kernel(
         consts = ctx.enter_context(tc.tile_pool(name="consts", bufs=1))
         resident = ctx.enter_context(tc.tile_pool(name="resident", bufs=1))
         stage = ctx.enter_context(tc.tile_pool(name="stage", bufs=2))
+        quantised = ctx.enter_context(tc.tile_pool(name="quantised", bufs=3))
         work = ctx.enter_context(tc.tile_pool(name="work", bufs=4))
         psum_turn = ctx.enter_context(tc.psum_pool(name="psum_turn", bufs=4))
         psum_rows = ctx.enter_context(tc.psum_pool(name="psum_rows", bufs=2))
@@ -82,12 +83,15 @@ def tile_vae_pb_t_kernel(
             nc.sync.dma_start(out=eps_sb[b - 1][:], in_=eps_blocks[b - 1])
         nc.sync.dma_start(out=eps_sb[BLOCKS - 1][:], in_=eps_blocks[BLOCKS - 1])
 
-        def turn_block(b):
+        def new_grouped():
             grouped = stage.tile([P, PASSES * BLOCK * PACK], BF16, name="grouped", align_bytes=64)
+            return grouped
+
+        def turn_row_tiles(b, tiles, grouped):
             grouped_words = grouped[:].bitcast(F32).rearrange(
                 "p (g c u) -> p g c u", g=PASSES, c=BLOCK, u=PAIRS
             )
-            for t in range(ROW_TILES):
+            for t in tiles:
                 hd_words = hd_sb[b][:, t, :].bitcast(F32)
                 turned = psum_turn.tile([P, PASSES * PAIRS, P], F32, name="turned", tag="turn")
                 for g in range(PASSES):
@@ -102,11 +106,10 @@ def tile_vae_pb_t_kernel(
                     out=grouped_words[:, :, t * P : (t + 1) * P, :],
                     in_=turned[:].rearrange("p (g u) c -> p g c u", u=PAIRS),
                 )
-            return grouped
 
         def quantise_block(grouped):
-            codes = stage.tile([P, PASSES, BLOCK], U32, name="codes", align_bytes=64)
-            hd_planes = stage.tile([P, PASSES, BLOCK], U8, name="hd_planes", align_bytes=64)
+            codes = quantised.tile([P, PASSES, BLOCK], U32, name="codes", align_bytes=64)
+            hd_planes = quantised.tile([P, PASSES, BLOCK], U8, name="hd_planes", align_bytes=64)
             nc.vector.quantize_mx(
                 out=codes[:].rearrange("p g c -> p (g c)").bitcast(FP8X4),
                 scales=hd_planes[:].rearrange("p g c -> p (g c)"),
@@ -125,9 +128,12 @@ def tile_vae_pb_t_kernel(
             nc.vector.tensor_copy(out=half_b_ls[:], in_=turned[:, 0:N_TILES])
             return half_b_ls
 
-        def std_of_block(codes, hd_planes, half_b_ls):
+        def new_std_turned():
             std_turned = stage.tile([P, N_TILES, BLOCK], F32, name="std_turned")
-            for j in range(N_TILES):
+            return std_turned
+
+        def std_of_outputs(n_tiles, codes, hd_planes, std_turned):
+            for j in n_tiles:
                 cols = slice(j * P, (j + 1) * P)
                 ls_turned = psum_turn.tile([P, BLOCK], F32, name="ls_turned", tag="turn")
                 for g in range(PASSES):
@@ -147,12 +153,9 @@ def tile_vae_pb_t_kernel(
                     bias=half_b_ls[:, j : j + 1],
                     scale=0.5,
                 )
-            return std_turned
 
-        def finish_row_tiles(b, tiles, codes, hd_planes, std_turned):
+        def std_back(tiles, std_turned):
             std_acc = {}
-            mu_acc = {}
-            noise = {}
             for t in tiles:
                 std_acc[t] = psum_rows.tile([P, N], F32, name="std_acc")
                 for j in range(N_TILES):
@@ -161,6 +164,10 @@ def tile_vae_pb_t_kernel(
                         std_turned[:, j, t * P : (t + 1) * P],
                         ident[:],
                     )
+            return std_acc
+
+        def mu_of_row_tiles(tiles, codes, hd_planes):
+            mu_acc = {}
             for t in tiles:
                 cols = slice(t * P, (t + 1) * P)
                 mu_acc[t] = psum_rows.tile([P, N], F32, name="mu_acc")
@@ -174,6 +181,10 @@ def tile_vae_pb_t_kernel(
                         start=(g == 0),
                         stop=(g == PASSES - 1),
                     )
+            return mu_acc
+
+        def finish_row_tiles(b, tiles, std_acc, mu_acc):
+            noise = {}
             for t in tiles:
                 noise[t] = work.tile([P, N], F32, name="noise")
                 nc.vector.tensor_tensor(
@@ -186,17 +197,28 @@ def tile_vae_pb_t_kernel(
                 nc.gpsimd.tensor_tensor(out=result[:], in0=summed[:], in1=b_mu_rows[:], op=ADD)
                 nc.sync.dma_start(out=out_blocks[b][:, t, :], in_=result[:])
 
+        halves = ((0, 1), (2, 3))
         with tc.manual_schedule():
-            grouped = {0: turn_block(0)}
+            grouped = {0: new_grouped()}
+            for tiles in halves:
+                turn_row_tiles(0, tiles, grouped[0])
             operands = {0: quantise_block(grouped[0])}
             half_b_ls = half_bias_per_partition()
-            grouped[1] = turn_block(1)
-            for b in range(BLOCKS):
-                codes, hd_planes = operands[b]
-                std_turned = std_of_block(codes, hd_planes, half_b_ls)
+            std_turned = {}
+            for b in range(-1, BLOCKS):
                 if b + 2 < BLOCKS:
-                    grouped[b + 2] = turn_block(b + 2)
-                finish_row_tiles(b, (0, 1), codes, hd_planes, std_turned)
+                    grouped[b + 2] = new_grouped()
                 if b + 1 < BLOCKS:
-                    operands[b + 1] = quantise_block(grouped[b + 1])
-                finish_row_tiles(b, (2, 3), codes, hd_planes, std_turned)
+                    std_turned[b + 1] = new_std_turned()
+                for tiles in halves:
+                    if b + 2 < BLOCKS:
+                        turn_row_tiles(b + 2, tiles, grouped[b + 2])
+                    if b >= 0:
+                        std_acc = std_back(tiles, std_turned[b])
+                        mu_acc = mu_of_row_tiles(tiles, *operands[b])
+                    if b + 1 < BLOCKS:
+                        std_of_outputs(tiles, *operands[b + 1], std_turned[b + 1])
+                    if b >= 0:
+                        finish_row_tiles(b, tiles, std_acc, mu_acc)
+                if b + 2 < BLOCKS:
+                    operands[b + 2] = quantise_block(grouped[b + 2])

@@ -22,8 +22,14 @@ ROW_TILES = 4
 BLOCK = P * ROW_TILES
 BLOCKS = ROWS // BLOCK
 N_TILES = N // P
+HALF = 2
+STEPS = BLOCKS * ROW_TILES // HALF
 MU, LS = 0, 1
 QUADRANTS = 4
+
+LS_LEAD = 2
+TURN_LEAD = 4
+SORT_LEAD = 5
 
 FLOPS = 2 * ROWS * K * (2 * N)
 
@@ -36,9 +42,14 @@ def tile_vae_pb_t_kernel(
     eps_blocks = eps_x.rearrange("(b p t) n -> b p t n", p=P, t=ROW_TILES)
     out_blocks = out.rearrange("(b p t) n -> b p t n", p=P, t=ROW_TILES)
 
+    def place(s):
+        first = (s % HALF) * HALF
+        return s // HALF, (first, first + 1)
+
     with ExitStack() as ctx:
         consts = ctx.enter_context(tc.tile_pool(name="consts", bufs=1))
         resident = ctx.enter_context(tc.tile_pool(name="resident", bufs=1))
+        sorting = ctx.enter_context(tc.tile_pool(name="sorting", bufs=2 * HALF))
         stage = ctx.enter_context(tc.tile_pool(name="stage", bufs=2))
         quantised = ctx.enter_context(tc.tile_pool(name="quantised", bufs=3))
         work = ctx.enter_context(tc.tile_pool(name="work", bufs=4))
@@ -59,63 +70,42 @@ def tile_vae_pb_t_kernel(
         nc.vector.memset(warm[:], 0.0)
         nc.scalar.activation(out=warm[:], in_=warm[:], func=EXP)
 
-        hd_sb = [resident.tile([P, ROW_TILES, K], BF16, name="hd%d" % b) for b in range(BLOCKS)]
+        hd_sb = [resident.tile([P, HALF, K], BF16, name="hd%d" % s) for s in range(STEPS)]
         eps_sb = [resident.tile([P, ROW_TILES, N], BF16, name="eps%d" % b) for b in range(BLOCKS)]
 
-        nc.sync.dma_start(out=hd_sb[0][:], in_=hd_blocks[0])
-        nc.sync.dma_start(out=b_ls_tiles[0:N_TILES, :], in_=b_ls_d.rearrange("(j c) -> j c", c=P))
-        for w, scales in ((LS, W_ls_d_scales), (MU, W_mu_d_scales)):
+        def load_hd(b):
+            for s in (HALF * b, HALF * b + 1):
+                tiles = place(s)[1]
+                nc.sync.dma_start(out=hd_sb[s][:], in_=hd_blocks[b][:, tiles[0] : tiles[1] + 1, :])
+
+        def load_weight(w, words, scales):
             for q in range(QUADRANTS):
                 nc.sync.dma_start(
                     out=w_planes[32 * q : 32 * q + 4, w, :, :].bitcast(I32),
                     in_=scales[:, 4 * q : 4 * q + 4, :].rearrange("g r n -> r g n").bitcast(I32),
                 )
-        for w, words in ((LS, W_ls_d_words), (MU, W_mu_d_words)):
             nc.sync.dma_start(
                 out=w_words[:, w, :, :].bitcast(I32),
                 in_=words.rearrange("g p n t -> p g (n t)").bitcast(I32),
             )
-        nc.sync.dma_start(out=hd_sb[1][:], in_=hd_blocks[1])
+
+        nc.sync.dma_start(out=b_ls_tiles[0:N_TILES, :], in_=b_ls_d.rearrange("(j c) -> j c", c=P))
+        load_hd(0)
+        load_weight(LS, W_ls_d_words, W_ls_d_scales)
+        load_hd(1)
+        load_weight(MU, W_mu_d_words, W_mu_d_scales)
         nc.sync.dma_start(out=eps_sb[0][:], in_=eps_blocks[0])
         nc.sync.dma_start(out=b_mu_rows[:], in_=b_mu_d.partition_broadcast(P))
         for b in range(2, BLOCKS):
-            nc.sync.dma_start(out=hd_sb[b][:], in_=hd_blocks[b])
+            load_hd(b)
             nc.sync.dma_start(out=eps_sb[b - 1][:], in_=eps_blocks[b - 1])
         nc.sync.dma_start(out=eps_sb[BLOCKS - 1][:], in_=eps_blocks[BLOCKS - 1])
 
-        def new_grouped():
-            grouped = stage.tile([P, PASSES * BLOCK * PACK], BF16, name="grouped", align_bytes=64)
-            return grouped
-
-        def turn_row_tiles(b, tiles, grouped):
-            grouped_words = grouped[:].bitcast(F32).rearrange(
-                "p (g c u) -> p g c u", g=PASSES, c=BLOCK, u=PAIRS
-            )
-            for t in tiles:
-                hd_words = hd_sb[b][:, t, :].bitcast(F32)
-                turned = psum_turn.tile([P, PASSES * PAIRS, P], F32, name="turned", tag="turn")
-                for g in range(PASSES):
-                    for u in range(PAIRS):
-                        words_of_pass = slice(g * P * PAIRS + u, (g + 1) * P * PAIRS, PAIRS)
-                        nc.tensor.transpose(
-                            turned[:, g * PAIRS + u, :],
-                            hd_words[:, words_of_pass],
-                            ident[:],
-                        )
-                nc.scalar.copy(
-                    out=grouped_words[:, :, t * P : (t + 1) * P, :],
-                    in_=turned[:].rearrange("p (g u) c -> p g c u", u=PAIRS),
-                )
-
-        def quantise_block(grouped):
-            codes = quantised.tile([P, PASSES, BLOCK], U32, name="codes", align_bytes=64)
-            hd_planes = quantised.tile([P, PASSES, BLOCK], U8, name="hd_planes", align_bytes=64)
-            nc.vector.quantize_mx(
-                out=codes[:].rearrange("p g c -> p (g c)").bitcast(FP8X4),
-                scales=hd_planes[:].rearrange("p g c -> p (g c)"),
-                in_=grouped[:],
-            )
-            return codes, hd_planes
+        sorted_words = {}
+        grouped = {}
+        codes = {}
+        hd_planes = {}
+        std_turned = {}
 
         def half_bias_per_partition():
             halved = consts.tile([P, P], F32, name="halved")
@@ -128,11 +118,54 @@ def tile_vae_pb_t_kernel(
             nc.vector.tensor_copy(out=half_b_ls[:], in_=turned[:, 0:N_TILES])
             return half_b_ls
 
-        def new_std_turned():
-            std_turned = stage.tile([P, N_TILES, BLOCK], F32, name="std_turned")
-            return std_turned
+        def sort_words(s):
+            b, tiles = place(s)
+            for t in tiles:
+                in_order = sorting.tile([P, PASSES, PAIRS, P], F32, name="in_order")
+                as_loaded = hd_sb[s][:, t % HALF, :].bitcast(F32).rearrange(
+                    "r (g p u) -> r g u p", g=PASSES, p=P, u=PAIRS
+                )
+                if t % 2 == 0:
+                    nc.vector.tensor_copy(out=in_order[:], in_=as_loaded)
+                else:
+                    nc.scalar.copy(out=in_order[:], in_=as_loaded)
+                sorted_words[(b, t)] = in_order
 
-        def std_of_outputs(n_tiles, codes, hd_planes, std_turned):
+        def turn(s):
+            b, tiles = place(s)
+            if b not in grouped:
+                grouped[b] = stage.tile([P, PASSES * BLOCK * PACK], BF16, name="grouped", align_bytes=64)
+            grouped_words = grouped[b][:].bitcast(F32).rearrange(
+                "p (g c u) -> p g c u", g=PASSES, c=BLOCK, u=PAIRS
+            )
+            for t in tiles:
+                turned = psum_turn.tile([P, PASSES, PAIRS, P], F32, name="turned", tag="turn")
+                for g in range(PASSES):
+                    for u in range(PAIRS):
+                        nc.tensor.transpose(turned[:, g, u, :], sorted_words[(b, t)][:, g, u, :], ident[:])
+                nc.scalar.copy(
+                    out=grouped_words[:, :, t * P : (t + 1) * P, :],
+                    in_=turned[:].rearrange("p g u c -> p g c u"),
+                )
+
+        def quantise(s):
+            b, tiles = place(s)
+            if b not in codes:
+                codes[b] = quantised.tile([P, PASSES, BLOCK], U32, name="codes", align_bytes=64)
+                hd_planes[b] = quantised.tile([P, PASSES, BLOCK], U8, name="hd_planes", align_bytes=64)
+            values = grouped[b][:].rearrange("p (g c k) -> p g c k", g=PASSES, c=BLOCK, k=PACK)
+            cols = slice(tiles[0] * P, (tiles[1] + 1) * P)
+            for g in range(PASSES):
+                nc.vector.quantize_mx(
+                    out=codes[b][:, g, cols].bitcast(FP8X4),
+                    scales=hd_planes[b][:, g, cols],
+                    in_=values[:, g, cols, :].rearrange("p c k -> p (c k)"),
+                )
+
+        def std_of_outputs(s, half_b_ls):
+            b, n_tiles = place(s)
+            if b not in std_turned:
+                std_turned[b] = stage.tile([P, N_TILES, BLOCK], F32, name="std_turned")
             for j in n_tiles:
                 cols = slice(j * P, (j + 1) * P)
                 ls_turned = psum_turn.tile([P, BLOCK], F32, name="ls_turned", tag="turn")
@@ -141,32 +174,34 @@ def tile_vae_pb_t_kernel(
                         out=ls_turned[:],
                         lhsT=w_words[:, LS, g, cols].bitcast(FP8X4),
                         lhsT_scale=w_planes[:, LS, g, cols],
-                        rhs=codes[:, g, :].bitcast(FP8X4),
-                        rhs_scale=hd_planes[:, g, :],
+                        rhs=codes[b][:, g, :].bitcast(FP8X4),
+                        rhs_scale=hd_planes[b][:, g, :],
                         start=(g == 0),
                         stop=(g == PASSES - 1),
                     )
                 nc.scalar.activation(
-                    out=std_turned[:, j, :],
+                    out=std_turned[b][:, j, :],
                     in_=ls_turned[:],
                     func=EXP,
                     bias=half_b_ls[:, j : j + 1],
                     scale=0.5,
                 )
 
-        def std_back(tiles, std_turned):
+        def std_back(s):
+            b, tiles = place(s)
             std_acc = {}
             for t in tiles:
                 std_acc[t] = psum_rows.tile([P, N], F32, name="std_acc")
                 for j in range(N_TILES):
                     nc.tensor.transpose(
                         std_acc[t][:, j * P : (j + 1) * P],
-                        std_turned[:, j, t * P : (t + 1) * P],
+                        std_turned[b][:, j, t * P : (t + 1) * P],
                         ident[:],
                     )
             return std_acc
 
-        def mu_of_row_tiles(tiles, codes, hd_planes):
+        def mu_of_rows(s):
+            b, tiles = place(s)
             mu_acc = {}
             for t in tiles:
                 cols = slice(t * P, (t + 1) * P)
@@ -174,8 +209,8 @@ def tile_vae_pb_t_kernel(
                 for g in range(PASSES):
                     nc.tensor.matmul_mx(
                         out=mu_acc[t][:],
-                        lhsT=codes[:, g, cols].bitcast(FP8X4),
-                        lhsT_scale=hd_planes[:, g, cols],
+                        lhsT=codes[b][:, g, cols].bitcast(FP8X4),
+                        lhsT_scale=hd_planes[b][:, g, cols],
                         rhs=w_words[:, MU, g, :].bitcast(FP8X4),
                         rhs_scale=w_planes[:, MU, g, :],
                         start=(g == 0),
@@ -183,7 +218,8 @@ def tile_vae_pb_t_kernel(
                     )
             return mu_acc
 
-        def finish_row_tiles(b, tiles, std_acc, mu_acc):
+        def finish(s, std_acc, mu_acc):
+            b, tiles = place(s)
             noise = {}
             for t in tiles:
                 noise[t] = work.tile([P, N], F32, name="noise")
@@ -197,28 +233,19 @@ def tile_vae_pb_t_kernel(
                 nc.gpsimd.tensor_tensor(out=result[:], in0=summed[:], in1=b_mu_rows[:], op=ADD)
                 nc.sync.dma_start(out=out_blocks[b][:, t, :], in_=result[:])
 
-        halves = ((0, 1), (2, 3))
         with tc.manual_schedule():
-            grouped = {0: new_grouped()}
-            for tiles in halves:
-                turn_row_tiles(0, tiles, grouped[0])
-            operands = {0: quantise_block(grouped[0])}
             half_b_ls = half_bias_per_partition()
-            std_turned = {}
-            for b in range(-1, BLOCKS):
-                if b + 2 < BLOCKS:
-                    grouped[b + 2] = new_grouped()
-                if b + 1 < BLOCKS:
-                    std_turned[b + 1] = new_std_turned()
-                for tiles in halves:
-                    if b + 2 < BLOCKS:
-                        turn_row_tiles(b + 2, tiles, grouped[b + 2])
-                    if b >= 0:
-                        std_acc = std_back(tiles, std_turned[b])
-                        mu_acc = mu_of_row_tiles(tiles, *operands[b])
-                    if b + 1 < BLOCKS:
-                        std_of_outputs(tiles, *operands[b + 1], std_turned[b + 1])
-                    if b >= 0:
-                        finish_row_tiles(b, tiles, std_acc, mu_acc)
-                if b + 2 < BLOCKS:
-                    operands[b + 2] = quantise_block(grouped[b + 2])
+            for s in range(-SORT_LEAD, STEPS):
+                if 0 <= s + TURN_LEAD < STEPS:
+                    turn(s + TURN_LEAD)
+                if s >= 0:
+                    std_acc = std_back(s)
+                    mu_acc = mu_of_rows(s)
+                if 0 <= s + LS_LEAD < STEPS:
+                    std_of_outputs(s + LS_LEAD, half_b_ls)
+                if s >= 0:
+                    finish(s, std_acc, mu_acc)
+                if 0 <= s + SORT_LEAD < STEPS:
+                    sort_words(s + SORT_LEAD)
+                if 0 <= s + TURN_LEAD < STEPS:
+                    quantise(s + TURN_LEAD)

@@ -238,6 +238,8 @@ def tile_vae_pb_t_kernel(
             for s in range(-SORT_LEAD, STEPS):
                 if 0 <= s + TURN_LEAD < STEPS:
                     turn(s + TURN_LEAD)
+                if 0 <= s + SORT_LEAD < STEPS:
+                    sort_words(s + SORT_LEAD)
                 if s >= 0:
                     std_acc = std_back(s)
                     mu_acc = mu_of_rows(s)
@@ -245,7 +247,5 @@ def tile_vae_pb_t_kernel(
                     std_of_outputs(s + LS_LEAD, half_b_ls)
                 if s >= 0:
                     finish(s, std_acc, mu_acc)
-                if 0 <= s + SORT_LEAD < STEPS:
-                    sort_words(s + SORT_LEAD)
                 if 0 <= s + TURN_LEAD < STEPS:
                     quantise(s + TURN_LEAD)

@@ -62,7 +62,7 @@ def tile_vae_pb_t_kernel(
         w_planes = consts.tile([P, 2, PASSES, N], U8, name="w_planes", align_bytes=64)
         nc.vector.memset(w_planes[:].bitcast(I32), 0)
         w_words = consts.tile([P, 2, PASSES, N], U32, name="w_words", align_bytes=64)
-        b_mu_rows = consts.tile([P, N], BF16, name="b_mu_rows")
+        b_mu_rows = consts.tile([P, HALF, N], BF16, name="b_mu_rows")
         b_ls_tiles = consts.tile([P, P], BF16, name="b_ls_tiles")
         nc.vector.memset(b_ls_tiles[:], 0.0)
 
@@ -95,7 +95,8 @@ def tile_vae_pb_t_kernel(
         load_hd(1)
         load_weight(MU, W_mu_d_words, W_mu_d_scales)
         nc.sync.dma_start(out=eps_sb[0][:], in_=eps_blocks[0])
-        nc.sync.dma_start(out=b_mu_rows[:], in_=b_mu_d.partition_broadcast(P))
+        nc.sync.dma_start(out=b_mu_rows[:, 0, :], in_=b_mu_d.partition_broadcast(P))
+        nc.vector.tensor_copy(out=b_mu_rows[:, 1, :], in_=b_mu_rows[:, 0, :])
         for b in range(2, BLOCKS):
             load_hd(b)
             nc.sync.dma_start(out=eps_sb[b - 1][:], in_=eps_blocks[b - 1])
@@ -226,12 +227,14 @@ def tile_vae_pb_t_kernel(
                 nc.vector.tensor_tensor(
                     out=noise[t][:], in0=std_acc[t][:], in1=eps_sb[b][:, t, :], op=MULT
                 )
+            summed = work.tile([P, HALF, N], F32, name="summed")
             for t in tiles:
-                summed = work.tile([P, N], F32, name="summed")
-                nc.vector.tensor_tensor(out=summed[:], in0=mu_acc[t][:], in1=noise[t][:], op=ADD)
-                result = work.tile([P, N], F32, name="result")
-                nc.gpsimd.tensor_tensor(out=result[:], in0=summed[:], in1=b_mu_rows[:], op=ADD)
-                nc.sync.dma_start(out=out_blocks[b][:, t, :], in_=result[:])
+                nc.vector.tensor_tensor(
+                    out=summed[:, t % HALF, :], in0=mu_acc[t][:], in1=noise[t][:], op=ADD
+                )
+            result = work.tile([P, HALF, N], F32, name="result")
+            nc.gpsimd.tensor_tensor(out=result[:], in0=summed[:], in1=b_mu_rows[:], op=ADD)
+            nc.sync.dma_start(out=out_blocks[b][:, tiles[0] : tiles[1] + 1, :], in_=result[:])
 
         with tc.manual_schedule():
             half_b_ls = half_bias_per_partition()

@@ -62,21 +62,31 @@ def tile_vae_pb_t_kernel(
         w_planes = consts.tile([P, 2, PASSES, N], U8, name="w_planes", align_bytes=64)
         nc.vector.memset(w_planes[:].bitcast(I32), 0)
         w_words = consts.tile([P, 2, PASSES, N], U32, name="w_words", align_bytes=64)
-        b_mu_rows = consts.tile([P, HALF, N], BF16, name="b_mu_rows")
         b_ls_tiles = consts.tile([P, P], BF16, name="b_ls_tiles")
         nc.vector.memset(b_ls_tiles[:], 0.0)
+        b_mu_row = consts.tile([P, N], BF16, name="b_mu_row")
+        nc.vector.memset(b_mu_row[:], 0.0)
+        ones = consts.tile([P, P], BF16, name="ones")
+        nc.vector.memset(ones[:], 1.0)
 
         warm = consts.tile([P, 1], F32, name="warm")
         nc.vector.memset(warm[:], 0.0)
         nc.scalar.activation(out=warm[:], in_=warm[:], func=EXP)
 
         hd_sb = [resident.tile([P, HALF, K], BF16, name="hd%d" % s) for s in range(STEPS)]
-        eps_sb = [resident.tile([P, ROW_TILES, N], BF16, name="eps%d" % b) for b in range(BLOCKS)]
+        eps_sb = [resident.tile([P, HALF, N], BF16, name="eps%d" % s) for s in range(STEPS)]
 
-        def load_hd(b):
-            for s in (HALF * b, HALF * b + 1):
-                tiles = place(s)[1]
-                nc.sync.dma_start(out=hd_sb[s][:], in_=hd_blocks[b][:, tiles[0] : tiles[1] + 1, :])
+        def load_hd(s, tiles_a_dma):
+            b, tiles = place(s)
+            for i in range(0, HALF, tiles_a_dma):
+                nc.sync.dma_start(
+                    out=hd_sb[s][:, i : i + tiles_a_dma, :],
+                    in_=hd_blocks[b][:, tiles[0] + i : tiles[0] + i + tiles_a_dma, :],
+                )
+
+        def load_eps(s):
+            b, tiles = place(s)
+            nc.sync.dma_start(out=eps_sb[s][:], in_=eps_blocks[b][:, tiles[0] : tiles[1] + 1, :])
 
         def load_weight(w, words, scales):
             for q in range(QUADRANTS):
@@ -89,18 +99,21 @@ def tile_vae_pb_t_kernel(
                 in_=words.rearrange("g p n t -> p g (n t)").bitcast(I32),
             )
 
-        nc.sync.dma_start(out=b_ls_tiles[0:N_TILES, :], in_=b_ls_d.rearrange("(j c) -> j c", c=P))
-        load_hd(0)
-        load_weight(LS, W_ls_d_words, W_ls_d_scales)
-        load_hd(1)
-        load_weight(MU, W_mu_d_words, W_mu_d_scales)
-        nc.sync.dma_start(out=eps_sb[0][:], in_=eps_blocks[0])
-        nc.sync.dma_start(out=b_mu_rows[:, 0, :], in_=b_mu_d.partition_broadcast(P))
-        nc.vector.tensor_copy(out=b_mu_rows[:, 1, :], in_=b_mu_rows[:, 0, :])
-        for b in range(2, BLOCKS):
-            load_hd(b)
-            nc.sync.dma_start(out=eps_sb[b - 1][:], in_=eps_blocks[b - 1])
-        nc.sync.dma_start(out=eps_sb[BLOCKS - 1][:], in_=eps_blocks[BLOCKS - 1])
+        def load_everything():
+            load_hd(0, 1)
+            nc.sync.dma_start(out=b_ls_tiles[0:N_TILES, :], in_=b_ls_d.rearrange("(j c) -> j c", c=P))
+            nc.sync.dma_start(out=b_mu_row[0:1, :], in_=b_mu_d.rearrange("(o n) -> o n", o=1))
+            load_hd(1, HALF)
+            load_hd(2, HALF)
+            load_weight(LS, W_ls_d_words, W_ls_d_scales)
+            for s in range(3, SORT_LEAD + 1):
+                load_hd(s, HALF)
+            load_eps(0)
+            load_weight(MU, W_mu_d_words, W_mu_d_scales)
+            for s in range(1, STEPS):
+                if s + SORT_LEAD < STEPS:
+                    load_hd(s + SORT_LEAD, HALF)
+                load_eps(s)
 
         sorted_words = {}
         grouped = {}
@@ -108,16 +121,21 @@ def tile_vae_pb_t_kernel(
         hd_planes = {}
         std_turned = {}
 
-        def half_bias_per_partition():
+        def spread_biases():
             halved = consts.tile([P, P], F32, name="halved")
             nc.vector.tensor_scalar(
                 out=halved[:], in0=b_ls_tiles[:], scalar1=0.5, scalar2=None, op0=MULT
             )
-            turned = psum_turn.tile([P, P], F32, name="bias_turned", tag="turn")
-            nc.tensor.transpose(turned[:], halved[:], ident[:])
+            bias_turned = psum_turn.tile([P, P], F32, name="bias_turned", tag="turn")
+            nc.tensor.transpose(bias_turned[:], halved[:], ident[:])
             half_b_ls = consts.tile([P, N_TILES], F32, name="half_b_ls")
-            nc.vector.tensor_copy(out=half_b_ls[:], in_=turned[:, 0:N_TILES])
-            return half_b_ls
+            nc.vector.tensor_copy(out=half_b_ls[:], in_=bias_turned[:, 0:N_TILES])
+            bias_spread = psum_turn.tile([P, N], F32, name="bias_spread", tag="turn")
+            nc.tensor.matmul(out=bias_spread[:], lhsT=ones[:], rhs=b_mu_row[:], start=True, stop=True)
+            b_mu_rows = consts.tile([P, HALF, N], BF16, name="b_mu_rows")
+            nc.vector.tensor_copy(out=b_mu_rows[:, 0, :], in_=bias_spread[:])
+            nc.vector.tensor_copy(out=b_mu_rows[:, 1, :], in_=b_mu_rows[:, 0, :])
+            return half_b_ls, b_mu_rows
 
         def sort_words(s):
             b, tiles = place(s)
@@ -219,13 +237,13 @@ def tile_vae_pb_t_kernel(
                     )
             return mu_acc
 
-        def finish(s, std_acc, mu_acc):
+        def finish(s, std_acc, mu_acc, b_mu_rows):
             b, tiles = place(s)
             noise = {}
             for t in tiles:
                 noise[t] = work.tile([P, N], F32, name="noise")
                 nc.vector.tensor_tensor(
-                    out=noise[t][:], in0=std_acc[t][:], in1=eps_sb[b][:, t, :], op=MULT
+                    out=noise[t][:], in0=std_acc[t][:], in1=eps_sb[s][:, t % HALF, :], op=MULT
                 )
             summed = work.tile([P, HALF, N], F32, name="summed")
             for t in tiles:
@@ -233,22 +251,32 @@ def tile_vae_pb_t_kernel(
                     out=summed[:, t % HALF, :], in0=mu_acc[t][:], in1=noise[t][:], op=ADD
                 )
             result = work.tile([P, HALF, N], F32, name="result")
-            nc.gpsimd.tensor_tensor(out=result[:], in0=summed[:], in1=b_mu_rows[:], op=ADD)
-            nc.sync.dma_start(out=out_blocks[b][:, tiles[0] : tiles[1] + 1, :], in_=result[:])
+            if s < STEPS - 1:
+                nc.gpsimd.tensor_tensor(out=result[:], in0=summed[:], in1=b_mu_rows[:], op=ADD)
+                nc.sync.dma_start(out=out_blocks[b][:, tiles[0] : tiles[1] + 1, :], in_=result[:])
+            else:
+                for t in tiles:
+                    i = t % HALF
+                    nc.vector.tensor_tensor(
+                        out=result[:, i, :], in0=summed[:, i, :], in1=b_mu_rows[:, i, :], op=ADD
+                    )
+                    nc.sync.dma_start(out=out_blocks[b][:, t, :], in_=result[:, i, :])
 
         with tc.manual_schedule():
-            half_b_ls = half_bias_per_partition()
+            load_everything()
             for s in range(-SORT_LEAD, STEPS):
                 if 0 <= s + TURN_LEAD < STEPS:
                     turn(s + TURN_LEAD)
                 if 0 <= s + SORT_LEAD < STEPS:
                     sort_words(s + SORT_LEAD)
+                if s == -TURN_LEAD:
+                    half_b_ls, b_mu_rows = spread_biases()
                 if s >= 0:
                     std_acc = std_back(s)
-                    mu_acc = mu_of_rows(s)
                 if 0 <= s + LS_LEAD < STEPS:
                     std_of_outputs(s + LS_LEAD, half_b_ls)
                 if s >= 0:
-                    finish(s, std_acc, mu_acc)
+                    mu_acc = mu_of_rows(s)
+                    finish(s, std_acc, mu_acc, b_mu_rows)
                 if 0 <= s + TURN_LEAD < STEPS:
                     quantise(s + TURN_LEAD)

@@ -29,7 +29,8 @@ QUADRANTS = 4
 
 LS_LEAD = 2
 TURN_LEAD = 4
-SORT_LEAD = 5
+SORT_LEAD = 6
+LOAD_LEAD = 5
 
 FLOPS = 2 * ROWS * K * (2 * N)
 
@@ -49,7 +50,7 @@ def tile_vae_pb_t_kernel(
     with ExitStack() as ctx:
         consts = ctx.enter_context(tc.tile_pool(name="consts", bufs=1))
         resident = ctx.enter_context(tc.tile_pool(name="resident", bufs=1))
-        sorting = ctx.enter_context(tc.tile_pool(name="sorting", bufs=2 * HALF))
+        sorting = ctx.enter_context(tc.tile_pool(name="sorting", bufs=3 * HALF))
         stage = ctx.enter_context(tc.tile_pool(name="stage", bufs=2))
         quantised = ctx.enter_context(tc.tile_pool(name="quantised", bufs=3))
         work = ctx.enter_context(tc.tile_pool(name="work", bufs=4))
@@ -106,13 +107,13 @@ def tile_vae_pb_t_kernel(
             load_hd(1, HALF)
             load_hd(2, HALF)
             load_weight(LS, W_ls_d_words, W_ls_d_scales)
-            for s in range(3, SORT_LEAD + 1):
+            for s in range(3, LOAD_LEAD + 1):
                 load_hd(s, HALF)
             load_eps(0)
             load_weight(MU, W_mu_d_words, W_mu_d_scales)
             for s in range(1, STEPS):
-                if s + SORT_LEAD < STEPS:
-                    load_hd(s + SORT_LEAD, HALF)
+                if s + LOAD_LEAD < STEPS:
+                    load_hd(s + LOAD_LEAD, HALF)
                 load_eps(s)
 
         sorted_words = {}
@@ -137,18 +138,17 @@ def tile_vae_pb_t_kernel(
             nc.vector.tensor_copy(out=b_mu_rows[:, 1, :], in_=b_mu_rows[:, 0, :])
             return half_b_ls, b_mu_rows
 
-        def sort_words(s):
+        def sort_words(s, i):
             b, tiles = place(s)
-            for t in tiles:
-                in_order = sorting.tile([P, PASSES, PAIRS, P], F32, name="in_order")
-                as_loaded = hd_sb[s][:, t % HALF, :].bitcast(F32).rearrange(
-                    "r (g p u) -> r g u p", g=PASSES, p=P, u=PAIRS
-                )
-                if t % 2 == 0:
-                    nc.vector.tensor_copy(out=in_order[:], in_=as_loaded)
-                else:
-                    nc.scalar.copy(out=in_order[:], in_=as_loaded)
-                sorted_words[(b, t)] = in_order
+            in_order = sorting.tile([P, PASSES, PAIRS, P], F32, name="in_order")
+            as_loaded = hd_sb[s][:, i, :].bitcast(F32).rearrange(
+                "r (g p u) -> r g u p", g=PASSES, p=P, u=PAIRS
+            )
+            if i == 0:
+                nc.vector.tensor_copy(out=in_order[:], in_=as_loaded)
+            else:
+                nc.scalar.copy(out=in_order[:], in_=as_loaded)
+            sorted_words[(b, tiles[i])] = in_order
 
         def turn(s):
             b, tiles = place(s)
@@ -237,7 +237,7 @@ def tile_vae_pb_t_kernel(
                     )
             return mu_acc
 
-        def finish(s, std_acc, mu_acc, b_mu_rows):
+        def products(s, std_acc):
             b, tiles = place(s)
             noise = {}
             for t in tiles:
@@ -245,14 +245,22 @@ def tile_vae_pb_t_kernel(
                 nc.vector.tensor_tensor(
                     out=noise[t][:], in0=std_acc[t][:], in1=eps_sb[s][:, t % HALF, :], op=MULT
                 )
+            return noise
+
+        def sums(s, noise, mu_acc, b_mu_rows):
+            b, tiles = place(s)
             summed = work.tile([P, HALF, N], F32, name="summed")
-            for t in tiles:
-                nc.vector.tensor_tensor(
-                    out=summed[:, t % HALF, :], in0=mu_acc[t][:], in1=noise[t][:], op=ADD
-                )
             result = work.tile([P, HALF, N], F32, name="result")
+            for t in tiles:
+                i = t % HALF
+                nc.vector.tensor_tensor(
+                    out=summed[:, i, :], in0=mu_acc[t][:], in1=noise[t][:], op=ADD
+                )
+                if s < STEPS - 1:
+                    nc.gpsimd.tensor_tensor(
+                        out=result[:, i, :], in0=summed[:, i, :], in1=b_mu_rows[:, i, :], op=ADD
+                    )
             if s < STEPS - 1:
-                nc.gpsimd.tensor_tensor(out=result[:], in0=summed[:], in1=b_mu_rows[:], op=ADD)
                 nc.sync.dma_start(out=out_blocks[b][:, tiles[0] : tiles[1] + 1, :], in_=result[:])
             else:
                 for t in tiles:
@@ -268,7 +276,7 @@ def tile_vae_pb_t_kernel(
                 if 0 <= s + TURN_LEAD < STEPS:
                     turn(s + TURN_LEAD)
                 if 0 <= s + SORT_LEAD < STEPS:
-                    sort_words(s + SORT_LEAD)
+                    sort_words(s + SORT_LEAD, 1)
                 if s == -TURN_LEAD:
                     half_b_ls, b_mu_rows = spread_biases()
                 if s >= 0:
@@ -277,6 +285,10 @@ def tile_vae_pb_t_kernel(
                     std_of_outputs(s + LS_LEAD, half_b_ls)
                 if s >= 0:
                     mu_acc = mu_of_rows(s)
-                    finish(s, std_acc, mu_acc, b_mu_rows)
+                    noise = products(s, std_acc)
                 if 0 <= s + TURN_LEAD < STEPS:
                     quantise(s + TURN_LEAD)
+                if 0 <= s + SORT_LEAD < STEPS:
+                    sort_words(s + SORT_LEAD, 0)
+                if s >= 0:
+                    sums(s, noise, mu_acc, b_mu_rows)

@@ -18,19 +18,16 @@ ROWS, K, N = 4096, 1024, 512
 PACK = 4
 PASSES = K // (P * PACK)
 PAIRS = 2
-ROW_TILES = 4
-BLOCK = P * ROW_TILES
-BLOCKS = ROWS // BLOCK
-N_TILES = N // P
 HALF = 2
-STEPS = BLOCKS * ROW_TILES // HALF
+STEP_ROWS = HALF * P
+STEPS = ROWS // STEP_ROWS
+N_TILES = N // P
 MU, LS = 0, 1
 QUADRANTS = 4
 
-LS_LEAD = 2
-TURN_LEAD = 4
-SORT_LEAD = 6
-LOAD_LEAD = 5
+LS_LEAD = 1
+TURN_LEAD = 2
+LOAD_LEAD = 3
 
 FLOPS = 2 * ROWS * K * (2 * N)
 
@@ -39,20 +36,15 @@ def tile_vae_pb_t_kernel(
     tc, hd, W_mu_d_words, W_mu_d_scales, b_mu_d, W_ls_d_words, W_ls_d_scales, b_ls_d, eps_x, out
 ):
     nc = tc.nc
-    hd_blocks = hd.rearrange("(b p t) k -> b p t k", p=P, t=ROW_TILES)
-    eps_blocks = eps_x.rearrange("(b p t) n -> b p t n", p=P, t=ROW_TILES)
-    out_blocks = out.rearrange("(b p t) n -> b p t n", p=P, t=ROW_TILES)
-
-    def place(s):
-        first = (s % HALF) * HALF
-        return s // HALF, (first, first + 1)
+    hd_steps = hd.rearrange("(s p i) k -> s p i k", p=P, i=HALF)
+    eps_steps = eps_x.rearrange("(s p i) n -> s p i n", p=P, i=HALF)
+    out_steps = out.rearrange("(s p i) n -> s p i n", p=P, i=HALF)
 
     with ExitStack() as ctx:
         consts = ctx.enter_context(tc.tile_pool(name="consts", bufs=1))
         resident = ctx.enter_context(tc.tile_pool(name="resident", bufs=1))
-        sorting = ctx.enter_context(tc.tile_pool(name="sorting", bufs=3 * HALF))
         stage = ctx.enter_context(tc.tile_pool(name="stage", bufs=2))
-        quantised = ctx.enter_context(tc.tile_pool(name="quantised", bufs=3))
+        quantised = ctx.enter_context(tc.tile_pool(name="quantised", bufs=4))
         work = ctx.enter_context(tc.tile_pool(name="work", bufs=4))
         psum_turn = ctx.enter_context(tc.psum_pool(name="psum_turn", bufs=4))
         psum_rows = ctx.enter_context(tc.psum_pool(name="psum_rows", bufs=2))
@@ -78,16 +70,13 @@ def tile_vae_pb_t_kernel(
         eps_sb = [resident.tile([P, HALF, N], BF16, name="eps%d" % s) for s in range(STEPS)]
 
         def load_hd(s, tiles_a_dma):
-            b, tiles = place(s)
             for i in range(0, HALF, tiles_a_dma):
                 nc.sync.dma_start(
-                    out=hd_sb[s][:, i : i + tiles_a_dma, :],
-                    in_=hd_blocks[b][:, tiles[0] + i : tiles[0] + i + tiles_a_dma, :],
+                    out=hd_sb[s][:, i : i + tiles_a_dma, :], in_=hd_steps[s][:, i : i + tiles_a_dma, :]
                 )
 
         def load_eps(s):
-            b, tiles = place(s)
-            nc.sync.dma_start(out=eps_sb[s][:], in_=eps_blocks[b][:, tiles[0] : tiles[1] + 1, :])
+            nc.sync.dma_start(out=eps_sb[s][:], in_=eps_steps[s])
 
         def load_weight(w, words, scales):
             for q in range(QUADRANTS):
@@ -104,19 +93,15 @@ def tile_vae_pb_t_kernel(
             load_hd(0, 1)
             nc.sync.dma_start(out=b_ls_tiles[0:N_TILES, :], in_=b_ls_d.rearrange("(j c) -> j c", c=P))
             nc.sync.dma_start(out=b_mu_row[0:1, :], in_=b_mu_d.rearrange("(o n) -> o n", o=1))
+            load_weight(LS, W_ls_d_words, W_ls_d_scales)
             load_hd(1, HALF)
             load_hd(2, HALF)
-            load_weight(LS, W_ls_d_words, W_ls_d_scales)
-            for s in range(3, LOAD_LEAD + 1):
-                load_hd(s, HALF)
-            load_eps(0)
             load_weight(MU, W_mu_d_words, W_mu_d_scales)
-            for s in range(1, STEPS):
+            for s in range(STEPS):
+                load_eps(s)
                 if s + LOAD_LEAD < STEPS:
                     load_hd(s + LOAD_LEAD, HALF)
-                load_eps(s)
 
-        sorted_words = {}
         grouped = {}
         codes = {}
         hd_planes = {}
@@ -138,98 +123,83 @@ def tile_vae_pb_t_kernel(
             nc.vector.tensor_copy(out=b_mu_rows[:, 1, :], in_=b_mu_rows[:, 0, :])
             return half_b_ls, b_mu_rows
 
-        def sort_words(s, i):
-            b, tiles = place(s)
-            in_order = sorting.tile([P, PASSES, PAIRS, P], F32, name="in_order")
-            as_loaded = hd_sb[s][:, i, :].bitcast(F32).rearrange(
-                "r (g p u) -> r g u p", g=PASSES, p=P, u=PAIRS
-            )
-            if i == 0:
-                nc.vector.tensor_copy(out=in_order[:], in_=as_loaded)
-            else:
-                nc.scalar.copy(out=in_order[:], in_=as_loaded)
-            sorted_words[(b, tiles[i])] = in_order
-
         def turn(s):
-            b, tiles = place(s)
-            if b not in grouped:
-                grouped[b] = stage.tile([P, PASSES * BLOCK * PACK], BF16, name="grouped", align_bytes=64)
-            grouped_words = grouped[b][:].bitcast(F32).rearrange(
-                "p (g c u) -> p g c u", g=PASSES, c=BLOCK, u=PAIRS
+            grouped[s] = stage.tile([P, PASSES * STEP_ROWS * PACK], BF16, name="grouped", align_bytes=64)
+            grouped_words = grouped[s][:].bitcast(F32).rearrange(
+                "p (g c u) -> p g c u", g=PASSES, c=STEP_ROWS, u=PAIRS
             )
-            for t in tiles:
+            for i in range(HALF):
                 turned = psum_turn.tile([P, PASSES, PAIRS, P], F32, name="turned", tag="turn")
+                words = hd_sb[s][:, i, :].bitcast(F32)
                 for g in range(PASSES):
                     for u in range(PAIRS):
-                        nc.tensor.transpose(turned[:, g, u, :], sorted_words[(b, t)][:, g, u, :], ident[:])
+                        nc.tensor.transpose(
+                            turned[:, g, u, :],
+                            words[:, PAIRS * P * g + u : PAIRS * P * (g + 1) : PAIRS],
+                            ident[:],
+                        )
                 nc.scalar.copy(
-                    out=grouped_words[:, :, t * P : (t + 1) * P, :],
+                    out=grouped_words[:, :, i * P : (i + 1) * P, :],
                     in_=turned[:].rearrange("p g u c -> p g c u"),
                 )
 
         def quantise(s):
-            b, tiles = place(s)
-            if b not in codes:
-                codes[b] = quantised.tile([P, PASSES, BLOCK], U32, name="codes", align_bytes=64)
-                hd_planes[b] = quantised.tile([P, PASSES, BLOCK], U8, name="hd_planes", align_bytes=64)
-            values = grouped[b][:].rearrange("p (g c k) -> p g c k", g=PASSES, c=BLOCK, k=PACK)
-            cols = slice(tiles[0] * P, (tiles[1] + 1) * P)
-            for g in range(PASSES):
-                nc.vector.quantize_mx(
-                    out=codes[b][:, g, cols].bitcast(FP8X4),
-                    scales=hd_planes[b][:, g, cols],
-                    in_=values[:, g, cols, :].rearrange("p c k -> p (c k)"),
-                )
+            codes[s] = quantised.tile([P, PASSES, STEP_ROWS], U32, name="codes", align_bytes=64)
+            hd_planes[s] = quantised.tile([P, PASSES, STEP_ROWS], U8, name="hd_planes", align_bytes=64)
+            nc.vector.quantize_mx(
+                out=codes[s][:].rearrange("p g c -> p (g c)").bitcast(FP8X4),
+                scales=hd_planes[s][:].rearrange("p g c -> p (g c)"),
+                in_=grouped[s][:],
+            )
 
         def std_of_outputs(s, half_b_ls):
-            b, n_tiles = place(s)
-            if b not in std_turned:
-                std_turned[b] = stage.tile([P, N_TILES, BLOCK], F32, name="std_turned")
-            for j in n_tiles:
-                cols = slice(j * P, (j + 1) * P)
-                ls_turned = psum_turn.tile([P, BLOCK], F32, name="ls_turned", tag="turn")
-                for g in range(PASSES):
-                    nc.tensor.matmul_mx(
-                        out=ls_turned[:],
-                        lhsT=w_words[:, LS, g, cols].bitcast(FP8X4),
-                        lhsT_scale=w_planes[:, LS, g, cols],
-                        rhs=codes[b][:, g, :].bitcast(FP8X4),
-                        rhs_scale=hd_planes[b][:, g, :],
-                        start=(g == 0),
-                        stop=(g == PASSES - 1),
+            std_turned[s] = stage.tile([P, N_TILES, STEP_ROWS], F32, name="std_turned")
+            for first in range(0, N_TILES, HALF):
+                ls_turned = psum_turn.tile([P, HALF, STEP_ROWS], F32, name="ls_turned", tag="turn")
+                for h in range(HALF):
+                    cols = slice((first + h) * P, (first + h + 1) * P)
+                    for g in range(PASSES):
+                        nc.tensor.matmul_mx(
+                            out=ls_turned[:, h, :],
+                            lhsT=w_words[:, LS, g, cols].bitcast(FP8X4),
+                            lhsT_scale=w_planes[:, LS, g, cols],
+                            rhs=codes[s][:, g, :].bitcast(FP8X4),
+                            rhs_scale=hd_planes[s][:, g, :],
+                            start=(g == 0),
+                            stop=(g == PASSES - 1),
+                        )
+                for h in range(HALF):
+                    j = first + h
+                    nc.scalar.activation(
+                        out=std_turned[s][:, j, :],
+                        in_=ls_turned[:, h, :],
+                        func=EXP,
+                        bias=half_b_ls[:, j : j + 1],
+                        scale=0.5,
                     )
-                nc.scalar.activation(
-                    out=std_turned[b][:, j, :],
-                    in_=ls_turned[:],
-                    func=EXP,
-                    bias=half_b_ls[:, j : j + 1],
-                    scale=0.5,
-                )
 
         def std_back(s):
-            b, tiles = place(s)
             std_acc = {}
-            for t in tiles:
-                std_acc[t] = psum_rows.tile([P, N], F32, name="std_acc")
+            for i in range(HALF):
+                std_acc[i] = psum_rows.tile([P, N], F32, name="std_acc")
                 for j in range(N_TILES):
                     nc.tensor.transpose(
-                        std_acc[t][:, j * P : (j + 1) * P],
-                        std_turned[b][:, j, t * P : (t + 1) * P],
+                        std_acc[i][:, j * P : (j + 1) * P],
+                        std_turned[s][:, j, i * P : (i + 1) * P],
                         ident[:],
                     )
             return std_acc
 
         def mu_of_rows(s):
-            b, tiles = place(s)
             mu_acc = {}
-            for t in tiles:
-                cols = slice(t * P, (t + 1) * P)
-                mu_acc[t] = psum_rows.tile([P, N], F32, name="mu_acc")
+            for i in range(HALF):
+                cols = slice(i * P, (i + 1) * P)
+                mu_acc[i] = psum_rows.tile([P, N], F32, name="mu_acc")
                 for g in range(PASSES):
                     nc.tensor.matmul_mx(
-                        out=mu_acc[t][:],
-                        lhsT=codes[b][:, g, cols].bitcast(FP8X4),
-                        lhsT_scale=hd_planes[b][:, g, cols],
+                        out=mu_acc[i][:],
+                        lhsT=codes[s][:, g, cols].bitcast(FP8X4),
+                        lhsT_scale=hd_planes[s][:, g, cols],
                         rhs=w_words[:, MU, g, :].bitcast(FP8X4),
                         rhs_scale=w_planes[:, MU, g, :],
                         start=(g == 0),
@@ -238,45 +208,35 @@ def tile_vae_pb_t_kernel(
             return mu_acc
 
         def products(s, std_acc):
-            b, tiles = place(s)
             noise = {}
-            for t in tiles:
-                noise[t] = work.tile([P, N], F32, name="noise")
-                nc.vector.tensor_tensor(
-                    out=noise[t][:], in0=std_acc[t][:], in1=eps_sb[s][:, t % HALF, :], op=MULT
-                )
+            for i in range(HALF):
+                noise[i] = work.tile([P, N], F32, name="noise")
+                nc.vector.tensor_tensor(out=noise[i][:], in0=std_acc[i][:], in1=eps_sb[s][:, i, :], op=MULT)
             return noise
 
         def sums(s, noise, mu_acc, b_mu_rows):
-            b, tiles = place(s)
             summed = work.tile([P, HALF, N], F32, name="summed")
             result = work.tile([P, HALF, N], F32, name="result")
-            for t in tiles:
-                i = t % HALF
-                nc.vector.tensor_tensor(
-                    out=summed[:, i, :], in0=mu_acc[t][:], in1=noise[t][:], op=ADD
-                )
+            for i in range(HALF):
+                nc.vector.tensor_tensor(out=summed[:, i, :], in0=mu_acc[i][:], in1=noise[i][:], op=ADD)
                 if s < STEPS - 1:
                     nc.gpsimd.tensor_tensor(
                         out=result[:, i, :], in0=summed[:, i, :], in1=b_mu_rows[:, i, :], op=ADD
                     )
             if s < STEPS - 1:
-                nc.sync.dma_start(out=out_blocks[b][:, tiles[0] : tiles[1] + 1, :], in_=result[:])
+                nc.sync.dma_start(out=out_steps[s], in_=result[:])
             else:
-                for t in tiles:
-                    i = t % HALF
+                for i in range(HALF):
                     nc.vector.tensor_tensor(
                         out=result[:, i, :], in0=summed[:, i, :], in1=b_mu_rows[:, i, :], op=ADD
                     )
-                    nc.sync.dma_start(out=out_blocks[b][:, t, :], in_=result[:, i, :])
+                    nc.sync.dma_start(out=out_steps[s][:, i, :], in_=result[:, i, :])
 
         with tc.manual_schedule():
             load_everything()
-            for s in range(-SORT_LEAD, STEPS):
+            for s in range(-TURN_LEAD, STEPS):
                 if 0 <= s + TURN_LEAD < STEPS:
                     turn(s + TURN_LEAD)
-                if 0 <= s + SORT_LEAD < STEPS:
-                    sort_words(s + SORT_LEAD, 1)
                 if s == -TURN_LEAD:
                     half_b_ls, b_mu_rows = spread_biases()
                 if s >= 0:
@@ -288,7 +248,5 @@ def tile_vae_pb_t_kernel(
                     noise = products(s, std_acc)
                 if 0 <= s + TURN_LEAD < STEPS:
                     quantise(s + TURN_LEAD)
-                if 0 <= s + SORT_LEAD < STEPS:
-                    sort_words(s + SORT_LEAD, 0)
                 if s >= 0:
                     sums(s, noise, mu_acc, b_mu_rows)

@@ -27,6 +27,7 @@ QUADRANTS = 4
 
 LS_LEAD = 1
 TURN_LEAD = 2
+SORT_LEAD = 3
 LOAD_LEAD = 3
 
 FLOPS = 2 * ROWS * K * (2 * N)
@@ -43,6 +44,7 @@ def tile_vae_pb_t_kernel(
     with ExitStack() as ctx:
         consts = ctx.enter_context(tc.tile_pool(name="consts", bufs=1))
         resident = ctx.enter_context(tc.tile_pool(name="resident", bufs=1))
+        sorting = ctx.enter_context(tc.tile_pool(name="sorting", bufs=3))
         stage = ctx.enter_context(tc.tile_pool(name="stage", bufs=2))
         quantised = ctx.enter_context(tc.tile_pool(name="quantised", bufs=4))
         work = ctx.enter_context(tc.tile_pool(name="work", bufs=4))
@@ -102,6 +104,7 @@ def tile_vae_pb_t_kernel(
                 if s + LOAD_LEAD < STEPS:
                     load_hd(s + LOAD_LEAD, HALF)
 
+        sorted_words = {}
         grouped = {}
         codes = {}
         hd_planes = {}
@@ -123,6 +126,13 @@ def tile_vae_pb_t_kernel(
             nc.vector.tensor_copy(out=b_mu_rows[:, 1, :], in_=b_mu_rows[:, 0, :])
             return half_b_ls, b_mu_rows
 
+        def sort_words(s):
+            sorted_words[s] = sorting.tile([P, PASSES, PAIRS, P], F32, name="in_order")
+            nc.scalar.copy(
+                out=sorted_words[s][:],
+                in_=hd_sb[s][:, 1, :].bitcast(F32).rearrange("r (g p u) -> r g u p", g=PASSES, p=P, u=PAIRS),
+            )
+
         def turn(s):
             grouped[s] = stage.tile([P, PASSES * STEP_ROWS * PACK], BF16, name="grouped", align_bytes=64)
             grouped_words = grouped[s][:].bitcast(F32).rearrange(
@@ -133,11 +143,11 @@ def tile_vae_pb_t_kernel(
                 words = hd_sb[s][:, i, :].bitcast(F32)
                 for g in range(PASSES):
                     for u in range(PAIRS):
-                        nc.tensor.transpose(
-                            turned[:, g, u, :],
-                            words[:, PAIRS * P * g + u : PAIRS * P * (g + 1) : PAIRS],
-                            ident[:],
-                        )
+                        if i == 0:
+                            run = words[:, PAIRS * P * g + u : PAIRS * P * (g + 1) : PAIRS]
+                        else:
+                            run = sorted_words[s][:, g, u, :]
+                        nc.tensor.transpose(turned[:, g, u, :], run, ident[:])
                 nc.scalar.copy(
                     out=grouped_words[:, :, i * P : (i + 1) * P, :],
                     in_=turned[:].rearrange("p g u c -> p g c u"),
@@ -234,9 +244,11 @@ def tile_vae_pb_t_kernel(
 
         with tc.manual_schedule():
             load_everything()
-            for s in range(-TURN_LEAD, STEPS):
+            for s in range(-SORT_LEAD, STEPS):
                 if 0 <= s + TURN_LEAD < STEPS:
                     turn(s + TURN_LEAD)
+                if 0 <= s + SORT_LEAD < STEPS:
+                    sort_words(s + SORT_LEAD)
                 if s == -TURN_LEAD:
                     half_b_ls, b_mu_rows = spread_biases()
                 if s >= 0:

@@ -109,6 +109,8 @@ def tile_vae_pb_t_kernel(
         codes = {}
         hd_planes = {}
         std_turned = {}
+        summed = {}
+        result = {}
 
         def spread_biases():
             halved = consts.tile([P, P], F32, name="halved")
@@ -225,22 +227,26 @@ def tile_vae_pb_t_kernel(
             return noise
 
         def sums(s, noise, mu_acc, b_mu_rows):
-            summed = work.tile([P, HALF, N], F32, name="summed")
-            result = work.tile([P, HALF, N], F32, name="result")
+            summed[s] = work.tile([P, HALF, N], F32, name="summed")
+            result[s] = work.tile([P, HALF, N], F32, name="result")
             for i in range(HALF):
-                nc.vector.tensor_tensor(out=summed[:, i, :], in0=mu_acc[i][:], in1=noise[i][:], op=ADD)
-                if s < STEPS - 1:
+                nc.vector.tensor_tensor(out=summed[s][:, i, :], in0=mu_acc[i][:], in1=noise[i][:], op=ADD)
+                if i == 0 and s < STEPS - 1:
                     nc.gpsimd.tensor_tensor(
-                        out=result[:, i, :], in0=summed[:, i, :], in1=b_mu_rows[:, i, :], op=ADD
+                        out=result[s][:, 0, :], in0=summed[s][:, 0, :], in1=b_mu_rows[:, 0, :], op=ADD
                     )
-            if s < STEPS - 1:
-                nc.sync.dma_start(out=out_steps[s], in_=result[:])
-            else:
+            if s == STEPS - 1:
                 for i in range(HALF):
                     nc.vector.tensor_tensor(
-                        out=result[:, i, :], in0=summed[:, i, :], in1=b_mu_rows[:, i, :], op=ADD
+                        out=result[s][:, i, :], in0=summed[s][:, i, :], in1=b_mu_rows[:, i, :], op=ADD
                     )
-                    nc.sync.dma_start(out=out_steps[s][:, i, :], in_=result[:, i, :])
+                    nc.sync.dma_start(out=out_steps[s][:, i, :], in_=result[s][:, i, :])
+
+        def second_bias(s, b_mu_rows):
+            nc.vector.tensor_tensor(
+                out=result[s][:, 1, :], in0=summed[s][:, 1, :], in1=b_mu_rows[:, 1, :], op=ADD
+            )
+            nc.sync.dma_start(out=out_steps[s], in_=result[s][:])
 
         with tc.manual_schedule():
             load_everything()
@@ -260,5 +266,7 @@ def tile_vae_pb_t_kernel(
                     noise = products(s, std_acc)
                 if 0 <= s + TURN_LEAD < STEPS:
                     quantise(s + TURN_LEAD)
+                if s >= 1:
+                    second_bias(s - 1, b_mu_rows)
                 if s >= 0:
                     sums(s, noise, mu_acc, b_mu_rows)

@@ -28,6 +28,7 @@ QUADRANTS = 4
 LS_LEAD = 1
 TURN_LEAD = 2
 SORT_LEAD = 3
+UNSORTED = 2
 LOAD_LEAD = 3
 
 FLOPS = 2 * ROWS * K * (2 * N)
@@ -44,7 +45,7 @@ def tile_vae_pb_t_kernel(
     with ExitStack() as ctx:
         consts = ctx.enter_context(tc.tile_pool(name="consts", bufs=1))
         resident = ctx.enter_context(tc.tile_pool(name="resident", bufs=1))
-        sorting = ctx.enter_context(tc.tile_pool(name="sorting", bufs=3))
+        sorting = ctx.enter_context(tc.tile_pool(name="sorting", bufs=3 * HALF))
         stage = ctx.enter_context(tc.tile_pool(name="stage", bufs=2))
         quantised = ctx.enter_context(tc.tile_pool(name="quantised", bufs=4))
         work = ctx.enter_context(tc.tile_pool(name="work", bufs=4))
@@ -129,11 +130,12 @@ def tile_vae_pb_t_kernel(
             return half_b_ls, b_mu_rows
 
         def sort_words(s):
-            sorted_words[s] = sorting.tile([P, PASSES, PAIRS, P], F32, name="in_order")
-            nc.scalar.copy(
-                out=sorted_words[s][:],
-                in_=hd_sb[s][:, 1, :].bitcast(F32).rearrange("r (g p u) -> r g u p", g=PASSES, p=P, u=PAIRS),
-            )
+            for i in range(HALF):
+                sorted_words[(s, i)] = sorting.tile([P, PASSES, PAIRS, P], F32, name="in_order")
+                nc.scalar.copy(
+                    out=sorted_words[(s, i)][:],
+                    in_=hd_sb[s][:, i, :].bitcast(F32).rearrange("r (g p u) -> r g u p", g=PASSES, p=P, u=PAIRS),
+                )
 
         def turn(s):
             grouped[s] = stage.tile([P, PASSES * STEP_ROWS * PACK], BF16, name="grouped", align_bytes=64)
@@ -145,10 +147,10 @@ def tile_vae_pb_t_kernel(
                 words = hd_sb[s][:, i, :].bitcast(F32)
                 for g in range(PASSES):
                     for u in range(PAIRS):
-                        if i == 0:
+                        if s < UNSORTED:
                             run = words[:, PAIRS * P * g + u : PAIRS * P * (g + 1) : PAIRS]
                         else:
-                            run = sorted_words[s][:, g, u, :]
+                            run = sorted_words[(s, i)][:, g, u, :]
                         nc.tensor.transpose(turned[:, g, u, :], run, ident[:])
                 nc.scalar.copy(
                     out=grouped_words[:, :, i * P : (i + 1) * P, :],
@@ -250,10 +252,10 @@ def tile_vae_pb_t_kernel(
 
         with tc.manual_schedule():
             load_everything()
-            for s in range(-SORT_LEAD, STEPS):
+            for s in range(-TURN_LEAD, STEPS):
                 if 0 <= s + TURN_LEAD < STEPS:
                     turn(s + TURN_LEAD)
-                if 0 <= s + SORT_LEAD < STEPS:
+                if UNSORTED <= s + SORT_LEAD < STEPS:
                     sort_words(s + SORT_LEAD)
                 if s == -TURN_LEAD:
                     half_b_ls, b_mu_rows = spread_biases()

@@ -82,22 +82,22 @@ def tile_vae_pb_t_kernel(
             nc.sync.dma_start(out=eps_sb[s][:], in_=eps_steps[s])
 
         def load_weight(w, words, scales):
+            nc.sync.dma_start(
+                out=w_words[:, w, :, :].bitcast(I32),
+                in_=words.rearrange("g p n t -> p g (n t)").bitcast(I32),
+            )
             for q in range(QUADRANTS):
                 nc.sync.dma_start(
                     out=w_planes[32 * q : 32 * q + 4, w, :, :].bitcast(I32),
                     in_=scales[:, 4 * q : 4 * q + 4, :].rearrange("g r n -> r g n").bitcast(I32),
                 )
-            nc.sync.dma_start(
-                out=w_words[:, w, :, :].bitcast(I32),
-                in_=words.rearrange("g p n t -> p g (n t)").bitcast(I32),
-            )
 
         def load_everything():
             load_hd(0, 1)
-            nc.sync.dma_start(out=b_ls_tiles[0:N_TILES, :], in_=b_ls_d.rearrange("(j c) -> j c", c=P))
-            nc.sync.dma_start(out=b_mu_row[0:1, :], in_=b_mu_d.rearrange("(o n) -> o n", o=1))
             load_weight(LS, W_ls_d_words, W_ls_d_scales)
+            nc.sync.dma_start(out=b_ls_tiles[0:N_TILES, :], in_=b_ls_d.rearrange("(j c) -> j c", c=P))
             load_hd(1, HALF)
+            nc.sync.dma_start(out=b_mu_row[0:1, :], in_=b_mu_d.rearrange("(o n) -> o n", o=1))
             load_hd(2, HALF)
             load_weight(MU, W_mu_d_words, W_mu_d_scales)
             for s in range(STEPS):
@@ -113,7 +113,7 @@ def tile_vae_pb_t_kernel(
         summed = {}
         result = {}
 
-        def spread_biases():
+        def spread_b_ls():
             halved = consts.tile([P, P], F32, name="halved")
             nc.vector.tensor_scalar(
                 out=halved[:], in0=b_ls_tiles[:], scalar1=0.5, scalar2=None, op0=MULT
@@ -122,12 +122,15 @@ def tile_vae_pb_t_kernel(
             nc.tensor.transpose(bias_turned[:], halved[:], ident[:])
             half_b_ls = consts.tile([P, N_TILES], F32, name="half_b_ls")
             nc.vector.tensor_copy(out=half_b_ls[:], in_=bias_turned[:, 0:N_TILES])
+            return half_b_ls
+
+        def spread_b_mu():
             bias_spread = psum_turn.tile([P, N], F32, name="bias_spread", tag="turn")
             nc.tensor.matmul(out=bias_spread[:], lhsT=ones[:], rhs=b_mu_row[:], start=True, stop=True)
             b_mu_rows = consts.tile([P, HALF, N], BF16, name="b_mu_rows")
             nc.vector.tensor_copy(out=b_mu_rows[:, 0, :], in_=bias_spread[:])
             nc.vector.tensor_copy(out=b_mu_rows[:, 1, :], in_=b_mu_rows[:, 0, :])
-            return half_b_ls, b_mu_rows
+            return b_mu_rows
 
         def sort_words(s):
             for i in range(HALF):
@@ -258,7 +261,7 @@ def tile_vae_pb_t_kernel(
                 if UNSORTED <= s + SORT_LEAD < STEPS:
                     sort_words(s + SORT_LEAD)
                 if s == -TURN_LEAD:
-                    half_b_ls, b_mu_rows = spread_biases()
+                    half_b_ls = spread_b_ls()
                 if s >= 0:
                     std_acc = std_back(s)
                 if 0 <= s + LS_LEAD < STEPS:
@@ -268,6 +271,8 @@ def tile_vae_pb_t_kernel(
                     noise = products(s, std_acc)
                 if 0 <= s + TURN_LEAD < STEPS:
                     quantise(s + TURN_LEAD)
+                if s == -LS_LEAD:
+                    b_mu_rows = spread_b_mu()
                 if s >= 1:
                     second_bias(s - 1, b_mu_rows)
                 if s >= 0:

@@ -26,6 +26,7 @@ MU, LS = 0, 1
 QUADRANTS = 4
 
 LS_LEAD = 1
+MU_LAG = 1
 TURN_LEAD = 2
 SORT_LEAD = 3
 UNSORTED = 2
@@ -47,8 +48,9 @@ def tile_vae_pb_t_kernel(
         resident = ctx.enter_context(tc.tile_pool(name="resident", bufs=1))
         sorting = ctx.enter_context(tc.tile_pool(name="sorting", bufs=3 * HALF))
         stage = ctx.enter_context(tc.tile_pool(name="stage", bufs=2))
-        quantised = ctx.enter_context(tc.tile_pool(name="quantised", bufs=4))
-        work = ctx.enter_context(tc.tile_pool(name="work", bufs=4))
+        quantised = ctx.enter_context(tc.tile_pool(name="quantised", bufs=5))
+        work = ctx.enter_context(tc.tile_pool(name="work", bufs=3 * HALF))
+        results = ctx.enter_context(tc.tile_pool(name="results", bufs=8))
         psum_turn = ctx.enter_context(tc.psum_pool(name="psum_turn", bufs=4))
         psum_rows = ctx.enter_context(tc.psum_pool(name="psum_rows", bufs=2))
 
@@ -110,8 +112,7 @@ def tile_vae_pb_t_kernel(
         codes = {}
         hd_planes = {}
         std_turned = {}
-        summed = {}
-        result = {}
+        biased = {}
 
         def spread_b_ls():
             halved = consts.tile([P, P], F32, name="halved")
@@ -127,9 +128,8 @@ def tile_vae_pb_t_kernel(
         def spread_b_mu():
             bias_spread = psum_turn.tile([P, N], F32, name="bias_spread", tag="turn")
             nc.tensor.matmul(out=bias_spread[:], lhsT=ones[:], rhs=b_mu_row[:], start=True, stop=True)
-            b_mu_rows = consts.tile([P, HALF, N], BF16, name="b_mu_rows")
-            nc.vector.tensor_copy(out=b_mu_rows[:, 0, :], in_=bias_spread[:])
-            nc.vector.tensor_copy(out=b_mu_rows[:, 1, :], in_=b_mu_rows[:, 0, :])
+            b_mu_rows = consts.tile([P, N], BF16, name="b_mu_rows")
+            nc.vector.tensor_copy(out=b_mu_rows[:], in_=bias_spread[:])
             return b_mu_rows
 
         def sort_words(s):
@@ -224,56 +224,42 @@ def tile_vae_pb_t_kernel(
                     )
             return mu_acc
 
-        def products(s, std_acc):
-            noise = {}
+        def products(s, std_acc, b_mu_rows):
             for i in range(HALF):
-                noise[i] = work.tile([P, N], F32, name="noise")
-                nc.vector.tensor_tensor(out=noise[i][:], in0=std_acc[i][:], in1=eps_sb[s][:, i, :], op=MULT)
-            return noise
+                noise = work.tile([P, N], F32, name="noise")
+                nc.vector.tensor_tensor(out=noise[:], in0=std_acc[i][:], in1=eps_sb[s][:, i, :], op=MULT)
+                biased[(s, i)] = work.tile([P, N], F32, name="biased")
+                nc.gpsimd.tensor_tensor(out=biased[(s, i)][:], in0=noise[:], in1=b_mu_rows[:], op=ADD)
 
-        def sums(s, noise, mu_acc, b_mu_rows):
-            summed[s] = work.tile([P, HALF, N], F32, name="summed")
-            result[s] = work.tile([P, HALF, N], F32, name="result")
+        def sums(s, mu_acc):
+            result = results.tile([P, HALF, N], F32, name="result")
             for i in range(HALF):
-                nc.vector.tensor_tensor(out=summed[s][:, i, :], in0=mu_acc[i][:], in1=noise[i][:], op=ADD)
-                if i == 0 and s < STEPS - 1:
-                    nc.gpsimd.tensor_tensor(
-                        out=result[s][:, 0, :], in0=summed[s][:, 0, :], in1=b_mu_rows[:, 0, :], op=ADD
-                    )
-            if s == STEPS - 1:
-                for i in range(HALF):
-                    nc.vector.tensor_tensor(
-                        out=result[s][:, i, :], in0=summed[s][:, i, :], in1=b_mu_rows[:, i, :], op=ADD
-                    )
-                    nc.sync.dma_start(out=out_steps[s][:, i, :], in_=result[s][:, i, :])
-
-        def second_bias(s, b_mu_rows):
-            nc.vector.tensor_tensor(
-                out=result[s][:, 1, :], in0=summed[s][:, 1, :], in1=b_mu_rows[:, 1, :], op=ADD
-            )
-            nc.sync.dma_start(out=out_steps[s], in_=result[s][:])
+                nc.vector.tensor_tensor(out=result[:, i, :], in0=mu_acc[i][:], in1=biased[(s, i)][:], op=ADD)
+                if s == STEPS - 1:
+                    nc.sync.dma_start(out=out_steps[s][:, i, :], in_=result[:, i, :])
+            if s < STEPS - 1:
+                nc.sync.dma_start(out=out_steps[s], in_=result[:])
 
         with tc.manual_schedule():
             load_everything()
-            for s in range(-TURN_LEAD, STEPS):
+            for s in range(-TURN_LEAD, STEPS + MU_LAG):
                 if 0 <= s + TURN_LEAD < STEPS:
                     turn(s + TURN_LEAD)
                 if UNSORTED <= s + SORT_LEAD < STEPS:
                     sort_words(s + SORT_LEAD)
                 if s == -TURN_LEAD:
                     half_b_ls = spread_b_ls()
-                if s >= 0:
+                if 0 <= s < STEPS:
                     std_acc = std_back(s)
                 if 0 <= s + LS_LEAD < STEPS:
                     std_of_outputs(s + LS_LEAD, half_b_ls)
-                if s >= 0:
-                    mu_acc = mu_of_rows(s)
-                    noise = products(s, std_acc)
-                if 0 <= s + TURN_LEAD < STEPS:
-                    quantise(s + TURN_LEAD)
                 if s == -LS_LEAD:
                     b_mu_rows = spread_b_mu()
-                if s >= 1:
-                    second_bias(s - 1, b_mu_rows)
-                if s >= 0:
-                    sums(s, noise, mu_acc, b_mu_rows)
+                if s - MU_LAG >= 0:
+                    mu_acc = mu_of_rows(s - MU_LAG)
+                if 0 <= s < STEPS:
+                    products(s, std_acc, b_mu_rows)
+                if 0 <= s + TURN_LEAD < STEPS:
+                    quantise(s + TURN_LEAD)
+                if s - MU_LAG >= 0:
+                    sums(s - MU_LAG, mu_acc)

@@ -29,7 +29,7 @@ LS_LEAD = 1
 MU_LAG = 1
 TURN_LEAD = 2
 SORT_LEAD = 3
-UNSORTED = 2
+UNSORTED = 4
 LOAD_LEAD = 3
 
 FLOPS = 2 * ROWS * K * (2 * N)
@@ -56,6 +56,8 @@ def tile_vae_pb_t_kernel(
 
         ident = consts.tile([P, P], F32, name="ident")
         make_identity(nc, ident[:])
+        ident_bf16 = consts.tile([P, P], BF16, name="ident_bf16")
+        make_identity(nc, ident_bf16[:])
 
         w_planes = consts.tile([P, 2, PASSES, N], U8, name="w_planes", align_bytes=64)
         nc.vector.memset(w_planes[:].bitcast(I32), 0)
@@ -96,9 +98,9 @@ def tile_vae_pb_t_kernel(
 
         def load_everything():
             load_hd(0, 1)
+            load_hd(1, HALF)
             load_weight(LS, W_ls_d_words, W_ls_d_scales)
             nc.sync.dma_start(out=b_ls_tiles[0:N_TILES, :], in_=b_ls_d.rearrange("(j c) -> j c", c=P))
-            load_hd(1, HALF)
             nc.sync.dma_start(out=b_mu_row[0:1, :], in_=b_mu_d.rearrange("(o n) -> o n", o=1))
             load_hd(2, HALF)
             load_weight(MU, W_mu_d_words, W_mu_d_scales)
@@ -115,14 +117,12 @@ def tile_vae_pb_t_kernel(
         biased = {}
 
         def spread_b_ls():
-            halved = consts.tile([P, P], F32, name="halved")
-            nc.vector.tensor_scalar(
-                out=halved[:], in0=b_ls_tiles[:], scalar1=0.5, scalar2=None, op0=MULT
-            )
-            bias_turned = psum_turn.tile([P, P], F32, name="bias_turned", tag="turn")
-            nc.tensor.transpose(bias_turned[:], halved[:], ident[:])
+            bias_turned = psum_turn.tile([P, P], BF16, name="bias_turned", tag="turn")
+            nc.tensor.transpose(bias_turned[:], b_ls_tiles[:], ident_bf16[:])
             half_b_ls = consts.tile([P, N_TILES], F32, name="half_b_ls")
-            nc.vector.tensor_copy(out=half_b_ls[:], in_=bias_turned[:, 0:N_TILES])
+            nc.vector.tensor_scalar(
+                out=half_b_ls[:], in0=bias_turned[:, 0:N_TILES], scalar1=0.5, scalar2=None, op0=MULT
+            )
             return half_b_ls
 
         def spread_b_mu():
@@ -247,14 +247,13 @@ def tile_vae_pb_t_kernel(
                     turn(s + TURN_LEAD)
                 if UNSORTED <= s + SORT_LEAD < STEPS:
                     sort_words(s + SORT_LEAD)
-                if s == -TURN_LEAD:
+                if s == -LS_LEAD:
                     half_b_ls = spread_b_ls()
+                    b_mu_rows = spread_b_mu()
                 if 0 <= s < STEPS:
                     std_acc = std_back(s)
                 if 0 <= s + LS_LEAD < STEPS:
                     std_of_outputs(s + LS_LEAD, half_b_ls)
-                if s == -LS_LEAD:
-                    b_mu_rows = spread_b_mu()
                 if s - MU_LAG >= 0:
                     mu_acc = mu_of_rows(s - MU_LAG)
                 if 0 <= s < STEPS:

@@ -85,11 +85,13 @@ def tile_vae_pb_t_kernel(
         def load_eps(s):
             nc.sync.dma_start(out=eps_sb[s][:], in_=eps_steps[s])
 
-        def load_weight(w, words, scales):
+        def load_words(w, words):
             nc.sync.dma_start(
                 out=w_words[:, w, :, :].bitcast(I32),
                 in_=words.rearrange("g p n t -> p g (n t)").bitcast(I32),
             )
+
+        def load_scales(w, scales):
             for q in range(QUADRANTS):
                 nc.sync.dma_start(
                     out=w_planes[32 * q : 32 * q + 4, w, :, :].bitcast(I32),
@@ -98,14 +100,18 @@ def tile_vae_pb_t_kernel(
 
         def load_everything():
             load_hd(0, 1)
-            load_hd(1, HALF)
-            load_weight(LS, W_ls_d_words, W_ls_d_scales)
+            load_scales(LS, W_ls_d_scales)
             nc.sync.dma_start(out=b_ls_tiles[0:N_TILES, :], in_=b_ls_d.rearrange("(j c) -> j c", c=P))
-            nc.sync.dma_start(out=b_mu_row[0:1, :], in_=b_mu_d.rearrange("(o n) -> o n", o=1))
+            load_hd(1, HALF)
+            load_words(LS, W_ls_d_words)
             load_hd(2, HALF)
-            load_weight(MU, W_mu_d_words, W_mu_d_scales)
+            nc.sync.dma_start(out=b_mu_row[0:1, :], in_=b_mu_d.rearrange("(o n) -> o n", o=1))
+            load_eps(0)
+            load_scales(MU, W_mu_d_scales)
+            load_words(MU, W_mu_d_words)
             for s in range(STEPS):
-                load_eps(s)
+                if s > 0:
+                    load_eps(s)
                 if s + LOAD_LEAD < STEPS:
                     load_hd(s + LOAD_LEAD, HALF)
 
@@ -211,7 +217,7 @@ def tile_vae_pb_t_kernel(
             mu_acc = {}
             for i in range(HALF):
                 cols = slice(i * P, (i + 1) * P)
-                mu_acc[i] = psum_rows.tile([P, N], F32, name="mu_acc")
+                mu_acc[i] = psum_rows.tile([P, N], F32, name="mu_acc", tag="std_acc" if s == STEPS - 1 else "mu_acc")
                 for g in range(PASSES):
                     nc.tensor.matmul_mx(
                         out=mu_acc[i][:],
@@ -234,9 +240,14 @@ def tile_vae_pb_t_kernel(
         def sums(s, mu_acc):
             result = results.tile([P, HALF, N], F32, name="result")
             for i in range(HALF):
-                nc.vector.tensor_tensor(out=result[:, i, :], in0=mu_acc[i][:], in1=biased[(s, i)][:], op=ADD)
-                if s == STEPS - 1:
-                    nc.sync.dma_start(out=out_steps[s][:, i, :], in_=result[:, i, :])
+                pieces = 2 if s == STEPS - 1 and i == 1 else 1
+                for c in range(0, N, N // pieces):
+                    cols = slice(c, c + N // pieces)
+                    nc.vector.tensor_tensor(
+                        out=result[:, i, cols], in0=mu_acc[i][:, cols], in1=biased[(s, i)][:, cols], op=ADD
+                    )
+                    if s == STEPS - 1:
+                        nc.sync.dma_start(out=out_steps[s][:, i, cols], in_=result[:, i, cols])
             if s < STEPS - 1:
                 nc.sync.dma_start(out=out_steps[s], in_=result[:])
 
@@ -249,6 +260,7 @@ def tile_vae_pb_t_kernel(
                     sort_words(s + SORT_LEAD)
                 if s == -LS_LEAD:
                     half_b_ls = spread_b_ls()
+                if s == 0:
                     b_mu_rows = spread_b_mu()
                 if 0 <= s < STEPS:
                     std_acc = std_back(s)

from contextlib import ExitStack

import concourse.mybir as mybir
from concourse.masks import make_identity

F32 = mybir.dt.float32
BF16 = mybir.dt.bfloat16
I32 = mybir.dt.int32
U32 = mybir.dt.uint32
U8 = mybir.dt.uint8
FP8X4 = mybir.dt.float8_e4m3fn_x4
ADD = mybir.AluOpType.add
MULT = mybir.AluOpType.mult
EXP = mybir.ActivationFunctionType.Exp

P = 128
ROWS, K, N = 4096, 1024, 512
PACK = 4
PASSES = K // (P * PACK)
PAIRS = 2
HALF = 2
STEP_ROWS = HALF * P
STEPS = ROWS // STEP_ROWS
N_TILES = N // P
MU, LS = 0, 1
QUADRANTS = 4

LS_LEAD = 1
MU_LAG = 1
TURN_LEAD = 2
SORT_LEAD = 3
UNSORTED = 4
LOAD_LEAD = 3

FLOPS = 2 * ROWS * K * (2 * N)


def tile_vae_pb_t_kernel(
    tc, hd, W_mu_d_words, W_mu_d_scales, b_mu_d, W_ls_d_words, W_ls_d_scales, b_ls_d, eps_x, out
):
    nc = tc.nc
    hd_steps = hd.rearrange("(s p i) k -> s p i k", p=P, i=HALF)
    eps_steps = eps_x.rearrange("(s p i) n -> s p i n", p=P, i=HALF)
    out_steps = out.rearrange("(s p i) n -> s p i n", p=P, i=HALF)

    with ExitStack() as ctx:
        consts = ctx.enter_context(tc.tile_pool(name="consts", bufs=1))
        resident = ctx.enter_context(tc.tile_pool(name="resident", bufs=1))
        sorting = ctx.enter_context(tc.tile_pool(name="sorting", bufs=3 * HALF))
        stage = ctx.enter_context(tc.tile_pool(name="stage", bufs=2))
        quantised = ctx.enter_context(tc.tile_pool(name="quantised", bufs=5))
        work = ctx.enter_context(tc.tile_pool(name="work", bufs=3 * HALF))
        results = ctx.enter_context(tc.tile_pool(name="results", bufs=8))
        psum_turn = ctx.enter_context(tc.psum_pool(name="psum_turn", bufs=4))
        psum_rows = ctx.enter_context(tc.psum_pool(name="psum_rows", bufs=2))

        ident = consts.tile([P, P], F32, name="ident")
        make_identity(nc, ident[:])
        ident_bf16 = consts.tile([P, P], BF16, name="ident_bf16")
        make_identity(nc, ident_bf16[:])

        w_planes = consts.tile([P, 2, PASSES, N], U8, name="w_planes", align_bytes=64)
        nc.vector.memset(w_planes[:].bitcast(I32), 0)
        w_words = consts.tile([P, 2, PASSES, N], U32, name="w_words", align_bytes=64)
        b_ls_tiles = consts.tile([P, P], BF16, name="b_ls_tiles")
        nc.vector.memset(b_ls_tiles[:], 0.0)
        b_mu_row = consts.tile([P, N], BF16, name="b_mu_row")
        nc.vector.memset(b_mu_row[:], 0.0)
        ones = consts.tile([P, P], BF16, name="ones")
        nc.vector.memset(ones[:], 1.0)

        warm = consts.tile([P, 1], F32, name="warm")
        nc.vector.memset(warm[:], 0.0)
        nc.scalar.activation(out=warm[:], in_=warm[:], func=EXP)

        hd_sb = [resident.tile([P, HALF, K], BF16, name="hd%d" % s) for s in range(STEPS)]
        eps_sb = [resident.tile([P, HALF, N], BF16, name="eps%d" % s) for s in range(STEPS)]

        def load_hd(s, tiles_a_dma):
            for i in range(0, HALF, tiles_a_dma):
                nc.sync.dma_start(
                    out=hd_sb[s][:, i : i + tiles_a_dma, :], in_=hd_steps[s][:, i : i + tiles_a_dma, :]
                )

        def load_eps(s):
            nc.sync.dma_start(out=eps_sb[s][:], in_=eps_steps[s])

        def load_words(w, words):
            nc.sync.dma_start(
                out=w_words[:, w, :, :].bitcast(I32),
                in_=words.rearrange("g p n t -> p g (n t)").bitcast(I32),
            )

        def load_scales(w, scales):
            for q in range(QUADRANTS):
                nc.sync.dma_start(
                    out=w_planes[32 * q : 32 * q + 4, w, :, :].bitcast(I32),
                    in_=scales[:, 4 * q : 4 * q + 4, :].rearrange("g r n -> r g n").bitcast(I32),
                )

        def load_everything():
            load_hd(0, 1)
            load_scales(LS, W_ls_d_scales)
            nc.sync.dma_start(out=b_ls_tiles[0:N_TILES, :], in_=b_ls_d.rearrange("(j c) -> j c", c=P))
            load_hd(1, HALF)
            load_words(LS, W_ls_d_words)
            load_hd(2, HALF)
            nc.sync.dma_start(out=b_mu_row[0:1, :], in_=b_mu_d.rearrange("(o n) -> o n", o=1))
            load_eps(0)
            load_scales(MU, W_mu_d_scales)
            load_words(MU, W_mu_d_words)
            for s in range(STEPS):
                if s > 0:
                    load_eps(s)
                if s + LOAD_LEAD < STEPS:
                    load_hd(s + LOAD_LEAD, HALF)

        sorted_words = {}
        grouped = {}
        codes = {}
        hd_planes = {}
        std_turned = {}
        biased = {}

        def spread_b_ls():
            bias_turned = psum_turn.tile([P, P], BF16, name="bias_turned", tag="turn")
            nc.tensor.transpose(bias_turned[:], b_ls_tiles[:], ident_bf16[:])
            half_b_ls = consts.tile([P, N_TILES], F32, name="half_b_ls")
            nc.vector.tensor_scalar(
                out=half_b_ls[:], in0=bias_turned[:, 0:N_TILES], scalar1=0.5, scalar2=None, op0=MULT
            )
            return half_b_ls

        def spread_b_mu():
            bias_spread = psum_turn.tile([P, N], F32, name="bias_spread", tag="turn")
            nc.tensor.matmul(out=bias_spread[:], lhsT=ones[:], rhs=b_mu_row[:], start=True, stop=True)
            b_mu_rows = consts.tile([P, N], BF16, name="b_mu_rows")
            nc.vector.tensor_copy(out=b_mu_rows[:], in_=bias_spread[:])
            return b_mu_rows

        def sort_words(s):
            for i in range(HALF):
                sorted_words[(s, i)] = sorting.tile([P, PASSES, PAIRS, P], F32, name="in_order")
                nc.scalar.copy(
                    out=sorted_words[(s, i)][:],
                    in_=hd_sb[s][:, i, :].bitcast(F32).rearrange("r (g p u) -> r g u p", g=PASSES, p=P, u=PAIRS),
                )

        def turn(s):
            grouped[s] = stage.tile([P, PASSES * STEP_ROWS * PACK], BF16, name="grouped", align_bytes=64)
            grouped_words = grouped[s][:].bitcast(F32).rearrange(
                "p (g c u) -> p g c u", g=PASSES, c=STEP_ROWS, u=PAIRS
            )
            for i in range(HALF):
                turned = psum_turn.tile([P, PASSES, PAIRS, P], F32, name="turned", tag="turn")
                words = hd_sb[s][:, i, :].bitcast(F32)
                for g in range(PASSES):
                    for u in range(PAIRS):
                        if s < UNSORTED:
                            run = words[:, PAIRS * P * g + u : PAIRS * P * (g + 1) : PAIRS]
                        else:
                            run = sorted_words[(s, i)][:, g, u, :]
                        nc.tensor.transpose(turned[:, g, u, :], run, ident[:])
                nc.scalar.copy(
                    out=grouped_words[:, :, i * P : (i + 1) * P, :],
                    in_=turned[:].rearrange("p g u c -> p g c u"),
                )

        def quantise(s):
            codes[s] = quantised.tile([P, PASSES, STEP_ROWS], U32, name="codes", align_bytes=64)
            hd_planes[s] = quantised.tile([P, PASSES, STEP_ROWS], U8, name="hd_planes", align_bytes=64)
            nc.vector.quantize_mx(
                out=codes[s][:].rearrange("p g c -> p (g c)").bitcast(FP8X4),
                scales=hd_planes[s][:].rearrange("p g c -> p (g c)"),
                in_=grouped[s][:],
            )

        def std_of_outputs(s, half_b_ls):
            std_turned[s] = stage.tile([P, N_TILES, STEP_ROWS], F32, name="std_turned")
            for first in range(0, N_TILES, HALF):
                ls_turned = psum_turn.tile([P, HALF, STEP_ROWS], F32, name="ls_turned", tag="turn")
                for h in range(HALF):
                    cols = slice((first + h) * P, (first + h + 1) * P)
                    for g in range(PASSES):
                        nc.tensor.matmul_mx(
                            out=ls_turned[:, h, :],
                            lhsT=w_words[:, LS, g, cols].bitcast(FP8X4),
                            lhsT_scale=w_planes[:, LS, g, cols],
                            rhs=codes[s][:, g, :].bitcast(FP8X4),
                            rhs_scale=hd_planes[s][:, g, :],
                            start=(g == 0),
                            stop=(g == PASSES - 1),
                        )
                for h in range(HALF):
                    j = first + h
                    nc.scalar.activation(
                        out=std_turned[s][:, j, :],
                        in_=ls_turned[:, h, :],
                        func=EXP,
                        bias=half_b_ls[:, j : j + 1],
                        scale=0.5,
                    )

        def std_back(s):
            std_acc = {}
            for i in range(HALF):
                std_acc[i] = psum_rows.tile([P, N], F32, name="std_acc")
                for j in range(N_TILES):
                    nc.tensor.transpose(
                        std_acc[i][:, j * P : (j + 1) * P],
                        std_turned[s][:, j, i * P : (i + 1) * P],
                        ident[:],
                    )
            return std_acc

        def mu_of_rows(s):
            mu_acc = {}
            for i in range(HALF):
                cols = slice(i * P, (i + 1) * P)
                mu_acc[i] = psum_rows.tile([P, N], F32, name="mu_acc", tag="std_acc" if s == STEPS - 1 else "mu_acc")
                for g in range(PASSES):
                    nc.tensor.matmul_mx(
                        out=mu_acc[i][:],
                        lhsT=codes[s][:, g, cols].bitcast(FP8X4),
                        lhsT_scale=hd_planes[s][:, g, cols],
                        rhs=w_words[:, MU, g, :].bitcast(FP8X4),
                        rhs_scale=w_planes[:, MU, g, :],
                        start=(g == 0),
                        stop=(g == PASSES - 1),
                    )
            return mu_acc

        def products(s, std_acc, b_mu_rows):
            for i in range(HALF):
                noise = work.tile([P, N], F32, name="noise")
                nc.vector.tensor_tensor(out=noise[:], in0=std_acc[i][:], in1=eps_sb[s][:, i, :], op=MULT)
                biased[(s, i)] = work.tile([P, N], F32, name="biased")
                nc.gpsimd.tensor_tensor(out=biased[(s, i)][:], in0=noise[:], in1=b_mu_rows[:], op=ADD)

        def sums(s, mu_acc):
            result = results.tile([P, HALF, N], F32, name="result")
            for i in range(HALF):
                pieces = 2 if s == STEPS - 1 and i == 1 else 1
                for c in range(0, N, N // pieces):
                    cols = slice(c, c + N // pieces)
                    nc.vector.tensor_tensor(
                        out=result[:, i, cols], in0=mu_acc[i][:, cols], in1=biased[(s, i)][:, cols], op=ADD
                    )
                    if s == STEPS - 1:
                        nc.sync.dma_start(out=out_steps[s][:, i, cols], in_=result[:, i, cols])
            if s < STEPS - 1:
                nc.sync.dma_start(out=out_steps[s], in_=result[:])

        with tc.manual_schedule():
            load_everything()
            for s in range(-TURN_LEAD, STEPS + MU_LAG):
                if 0 <= s + TURN_LEAD < STEPS:
                    turn(s + TURN_LEAD)
                if UNSORTED <= s + SORT_LEAD < STEPS:
                    sort_words(s + SORT_LEAD)
                if s == -LS_LEAD:
                    half_b_ls = spread_b_ls()
                if s == 0:
                    b_mu_rows = spread_b_mu()
                if 0 <= s < STEPS:
                    std_acc = std_back(s)
                if 0 <= s + LS_LEAD < STEPS:
                    std_of_outputs(s + LS_LEAD, half_b_ls)
                if s - MU_LAG >= 0:
                    mu_acc = mu_of_rows(s - MU_LAG)
                if 0 <= s < STEPS:
                    products(s, std_acc, b_mu_rows)
                if 0 <= s + TURN_LEAD < STEPS:
                    quantise(s + TURN_LEAD)
                if s - MU_LAG >= 0:
                    sums(s - MU_LAG, mu_acc)
